import numpy as np
import ml_dtypes


def mxq(x, axis, fmt="e4m3"):
    dtype, down = {"e4m3": (ml_dtypes.float8_e4m3fn, 7), "e5m2": (ml_dtypes.float8_e5m2, 14)}[fmt]
    v = np.moveaxis(np.asarray(x, np.float32).astype(ml_dtypes.bfloat16).astype(np.float64), axis, -1)
    blocks = v.reshape(v.shape[:-1] + (-1, 32))
    amax = np.abs(blocks).max(-1, keepdims=True)
    byte = np.maximum(np.where(amax > 0, np.frexp(amax)[1] - 1 + 127, 0) - down, 1)
    scale = np.exp2(byte - 127.0)
    codes = (blocks / scale).astype(np.float32).astype(dtype).astype(np.float64)
    return np.moveaxis((codes * scale).reshape(v.shape), -1, axis)


WIDE = False


def mx_kscale(k):
    if not WIDE:
        return np.ones(k)
    levels = np.array([10, -10, 5, -5, 0])
    if k % 512:
        return np.exp2(np.random.permutation(np.resize(levels, k // 32))).repeat(32)
    a = np.empty((k // 512, 16))
    for p in range(k // 512):
        a[p, :8] = np.random.permutation(np.resize(levels, 8))
        for g in range(8):
            far = levels[np.abs(levels - a[p, g]) >= 10]
            a[p, g + 8] = far[np.random.randint(len(far))]
    return np.exp2(a.ravel()).repeat(32)


BF16 = ml_dtypes.bfloat16


def bf(x):
    return np.asarray(x, np.float32).astype(BF16)


def f64(x):
    return np.asarray(x).astype(np.float64)


B, S, D, H, DH, F = 4, 1024, 1024, 4, 128, 512
E = H * DH
EPS = 1e-5
NTERMS = 120


def layernorm(x, g, b):
    mu = x.mean(-1, keepdims=True)
    var = np.square(x - mu).mean(-1, keepdims=True)
    return (x - mu) / np.sqrt(var + EPS) * g + b


def erf(v):
    a = np.minimum(np.maximum(v, -6.0), 6.0)
    term = a.copy()
    total = a.copy()
    for n in range(1, NTERMS):
        term = term * (2.0 * a * a) / (2.0 * n + 1.0)
        total = total + term
    return 2.0 / np.sqrt(np.pi) * np.exp(-a * a) * total


def gelu_erf(v):
    return 0.5 * v * (1.0 + erf(v / np.sqrt(2.0)))


def setup_inputs():
    s, t = mx_kscale(E), mx_kscale(D)
    x = np.random.standard_normal((B, S, D)) + 0.5 * np.random.standard_normal((B, S, 1))
    return {"h_attn": bf(0.2 * np.random.standard_normal((B, S, E)) * s),
            "x": bf(x),
            "w_out": bf(np.random.standard_normal((D, E)) * 2.0 / np.sqrt(E) / s),
            "w_fc1": bf(np.random.standard_normal((F, D)) / np.sqrt(D) / t),
            "g2": bf((1.0 + 0.1 * np.random.standard_normal(D)) * t),
            "b2": bf(0.1 * np.random.standard_normal(D) * t)}


def reference(h_attn, x, w_out, w_fc1, g2, b2):
    x_mid = f64(x) + (mxq(f64(h_attn), 2, "e4m3") @ mxq(f64(w_out), 1, "e4m3").T)
    h = layernorm(x_mid, f64(g2), f64(b2))
    u = mxq(h, 2, "e4m3") @ mxq(f64(w_fc1), 1, "e4m3").T
    return x_mid, gelu_erf(u)

@@ -1,0 +1,400 @@
+from contextlib import ExitStack
+
+import concourse.mybir as mybir
+from concourse.masks import make_identity
+
+F32 = mybir.dt.float32
+BF16 = mybir.dt.bfloat16
+U32 = mybir.dt.uint32
+U8 = mybir.dt.uint8
+FP8X4 = mybir.dt.float8_e4m3fn_x4
+ACT = mybir.ActivationFunctionType
+ALU = mybir.AluOpType
+
+P = 128
+TOKENS = 4096
+D = 1024
+E = 512
+F = 512
+EPS = 1e-5
+BANK = 512
+D_BLOCKS = D // P
+PASSES2 = D // 512
+LOAD_TILES = 4
+LOAD_TOKENS = LOAD_TILES * P
+LOADS = TOKENS // LOAD_TOKENS
+TILES = 2
+GROUP = TILES * P
+GROUPS = TOKENS // GROUP
+LOADS_AHEAD = 3
+
+FLOPS = 2 * TOKENS * E * D + 2 * TOKENS * D * F
+
+
+def tile_minitransformerlayer_pb_t_kernel(tc, h_attn, x, w_out, w_fc1, g2, b2, out_0, out_1):
+    nc = tc.nc
+    ha_rows = h_attn.flatten_outer_dims()
+    x_rows = x.flatten_outer_dims()
+    xmid_rows = out_0.flatten_outer_dims()
+    act_rows = out_1.flatten_outer_dims()
+
+    with ExitStack() as ctx:
+        ctx.enter_context(tc.manual_schedule())
+        const = ctx.enter_context(tc.tile_pool(name="const", bufs=1))
+        loads = ctx.enter_context(tc.tile_pool(name="loads", bufs=LOADS_AHEAD + 1))
+        work = ctx.enter_context(tc.tile_pool(name="work", bufs=2))
+        small = ctx.enter_context(tc.tile_pool(name="small", bufs=6))
+        accp = ctx.enter_context(tc.psum_pool(name="accp", bufs=5))
+        ztp = ctx.enter_context(tc.psum_pool(name="ztp", bufs=2))
+        htp = ctx.enter_context(tc.psum_pool(name="htp", bufs=1))
+
+        def load_view(rows, n):
+            return rows[n * LOAD_TOKENS : (n + 1) * LOAD_TOKENS, :].rearrange("(p j) c -> p j c", j=LOAD_TILES)
+
+        def group_view(rows, k):
+            first = (k % 2) * TILES
+            return load_view(rows, k // 2)[:, first : first + TILES, :]
+
+        ha_tiles = {}
+        x_tiles = {}
+
+        def load_h_attn(n):
+            ha_sb = loads.tile([P, LOAD_TILES * E], BF16, name="ha_sb")
+            nc.sync.dma_start(out=ha_sb[:].rearrange("p (j c) -> p j c", j=LOAD_TILES), in_=load_view(ha_rows, n))
+            ha_tiles[n] = ha_sb
+
+        def load_x(n):
+            x_sb = loads.tile([P, LOAD_TILES, D], BF16, name="x_sb")
+            nc.sync.dma_start(out=x_sb[:], in_=load_view(x_rows, n))
+            x_tiles[n] = x_sb
+
+        load_h_attn(0)
+        w1_raw = const.tile([P, D_BLOCKS * E], BF16)
+        w1_raw_blocks = w1_raw[:].rearrange("p (r k) -> p r k", k=E)
+        w_out_blocks = w_out.rearrange("(r p) k -> p r k", p=P)
+        for half in range(D // BANK):
+            blocks = slice(half * BANK // P, (half + 1) * BANK // P)
+            nc.sync.dma_start(out=w1_raw_blocks[:, blocks, :], in_=w_out_blocks[:, blocks, :])
+        load_x(0)
+        load_h_attn(1)
+        load_h_attn(2)
+        load_x(1)
+        gb_rows = const.tile([P, 512], BF16)
+        nc.vector.memset(gb_rows[:], 0.0)
+        nc.sync.dma_start(out=gb_rows[0:PASSES2, :], in_=g2.rearrange("(s k) -> s k", k=512))
+        nc.sync.dma_start(out=gb_rows[PASSES2 : 2 * PASSES2, :], in_=b2.rearrange("(s k) -> s k", k=512))
+        w2_raw = const.tile([P, F // P, D], BF16)
+        nc.sync.dma_start(out=w2_raw[:], in_=w_fc1.rearrange("(r p) k -> p r k", p=P))
+        load_x(2)
+
+        ident_f32 = const.tile([P, P], F32)
+        make_identity(nc, ident_f32[:])
+        ident_bf = const.tile([P, P], BF16)
+        make_identity(nc, ident_bf[:])
+        neg_half = const.tile([P, TILES], F32)
+        nc.gpsimd.memset(neg_half[:], -0.5)
+        warm = const.tile([P, 1], F32)
+        nc.vector.memset(warm[:], 0.0)
+        nc.scalar.activation(out=warm[:], in_=warm[:], func=ACT.Gelu)
+
+        w1_grp = const.tile([P, D * 4], BF16, align_bytes=64)
+        w1_grp_words = w1_grp[:].bitcast(F32).rearrange("p (d u) -> p d u", u=2)
+        w1_words = w1_raw[:].bitcast(F32)
+        w1_codes = const.tile([P, D], U32, align_bytes=64)
+        w1_scales = const.tile([P, D], U8, align_bytes=64)
+
+        def quantise_w_out():
+            for q in range(D_BLOCKS // 2):
+                w1_ps = ztp.tile([P, 2, 2 * P], F32, tag="ztp")
+                for rr in range(2):
+                    for u in range(2):
+                        row = 2 * q + rr
+                        words = w1_words[:, row * (E // 2) + u : (row + 1) * (E // 2) : 2]
+                        nc.tensor.transpose(w1_ps[:, u, rr * P : (rr + 1) * P], words, ident_f32[:])
+                w1_out = w1_grp_words[:, q * 2 * P : (q + 1) * 2 * P, :]
+                if q % 2 == 0:
+                    nc.vector.tensor_copy(out=w1_out, in_=w1_ps[:].rearrange("p u d -> p d u"))
+                else:
+                    nc.scalar.copy(out=w1_out, in_=w1_ps[:].rearrange("p u d -> p d u"))
+                    half = q // 2
+                    nc.vector.quantize_mx(
+                        out=w1_codes[:, half * BANK : (half + 1) * BANK].bitcast(FP8X4),
+                        scales=w1_scales[:, half * BANK : (half + 1) * BANK],
+                        in_=w1_grp[:, half * BANK * 4 : (half + 1) * BANK * 4],
+                    )
+
+        gb = const.tile([P, 4, 2 * PASSES2], F32)
+
+        def transpose_gain_and_bias():
+            gb_ps = ztp.tile([P, 4, P], BF16, tag="ztp")
+            for t in range(4):
+                nc.tensor.transpose(gb_ps[:, t, :], gb_rows[:, t:512:4], ident_bf[:])
+            nc.scalar.copy(out=gb[:], in_=gb_ps[:, :, 0 : 2 * PASSES2])
+
+        w2_grp = const.tile([P, PASSES2, F, 4], BF16, align_bytes=64)
+        w2_codes = const.tile([P, PASSES2, F], U32, align_bytes=64)
+        w2_scales = const.tile([P, PASSES2, F], U8, align_bytes=64)
+
+        def transpose_w_fc1(s, q):
+            w2_ps = ztp.tile([P, 4, 2 * P], BF16, tag="ztp")
+            for t in range(4):
+                for rr in range(2):
+                    nc.tensor.transpose(
+                        w2_ps[:, t, rr * P : (rr + 1) * P], w2_raw[:, 2 * q + rr, 512 * s + t : 512 * (s + 1) : 4], ident_bf[:]
+                    )
+            nc.scalar.copy(out=w2_grp[:, s, q * 2 * P : (q + 1) * 2 * P, :], in_=w2_ps[:].rearrange("p t f -> p f t"))
+
+        def quantise_w_fc1(s):
+            nc.vector.quantize_mx(
+                out=w2_codes[:, s, :].bitcast(FP8X4),
+                scales=w2_scales[:, s, :],
+                in_=w2_grp[:, s, :, :].rearrange("p f t -> p (f t)"),
+            )
+
+        h_banks = {}
+        h_groups = {}
+        h_ops = {}
+        acc1_banks = {}
+        xm_tiles = {}
+        mean_tiles = {}
+        z_tiles = {}
+        norm_tiles = {}
+        plane_tiles = {}
+        zgrp_tiles = {}
+        z_ops = {}
+        act_tiles = {}
+
+        def live(k):
+            return 0 <= k < GROUPS
+
+        def transpose_h_attn(k, h):
+            if h == 0:
+                h_banks[k] = htp.tile([P, 2, GROUP], F32, name="h_ps")
+            h_ps = h_banks[k]
+            ha_words = ha_tiles[k // 2][:].bitcast(F32)
+            for u in range(2):
+                row = (k % 2) * TILES + h
+                words = ha_words[:, row * (E // 2) + u : (row + 1) * (E // 2) : 2]
+                nc.tensor.transpose(h_ps[:, u, h * P : (h + 1) * P], words, ident_f32[:])
+            if h == TILES - 1:
+                h_grp = work.tile([P, GROUP * 4], BF16, align_bytes=64, name="h_grp", bufs=3)
+                nc.scalar.copy(
+                    out=h_grp[:].bitcast(F32).rearrange("p (r u) -> p r u", u=2), in_=h_ps[:].rearrange("p u r -> p r u")
+                )
+                h_groups[k] = h_grp
+
+        def quantise_h_attn(k):
+            h_codes = work.tile([P, GROUP], U32, align_bytes=64, name="h_codes", bufs=4)
+            h_scales = work.tile([P, GROUP], U8, align_bytes=64, name="h_scales", bufs=4)
+            nc.vector.quantize_mx(out=h_codes[:].bitcast(FP8X4), scales=h_scales[:], in_=h_groups[k][:])
+            h_ops[k] = (h_codes, h_scales)
+
+        def first_matmul(k, h):
+            h_codes, h_scales = h_ops[k]
+            tok = slice(h * P, (h + 1) * P)
+            for half in range(D // BANK):
+                cols = slice(half * BANK, (half + 1) * BANK)
+                acc1 = accp.tile([P, BANK], F32, tag="acc")
+                nc.tensor.matmul_mx(
+                    out=acc1[:],
+                    lhsT=h_codes[:, tok].bitcast(FP8X4),
+                    lhsT_scale=h_scales[:, tok],
+                    rhs=w1_codes[:, cols].bitcast(FP8X4),
+                    rhs_scale=w1_scales[:, cols],
+                    start=True,
+                    stop=True,
+                )
+                acc1_banks[(k, h, half)] = acc1
+
+        def add_residual(k, h, half):
+            if h == 0 and half == 0:
+                xm_tiles[k] = work.tile([P, TILES, D], F32, name="xm", bufs=4)
+                mean_tiles[k] = (
+                    small.tile([P, TILES, 2], F32, name="sums"),
+                    small.tile([P, TILES], F32, name="neg_mu"),
+                )
+            xm = xm_tiles[k]
+            sums = mean_tiles[k][0]
+            x_sb = x_tiles[k // 2]
+            cols = slice(half * BANK, (half + 1) * BANK)
+            nc.vector.scalar_tensor_tensor(
+                out=xm[:, h, cols],
+                in0=acc1_banks[(k, h, half)][:],
+                scalar=1.0,
+                in1=x_sb[:, (k % 2) * TILES + h, cols],
+                op0=ALU.mult,
+                op1=ALU.add,
+                accum_out=sums[:, h, half : half + 1],
+            )
+            if h == TILES - 1 and half == 1:
+                nc.sync.dma_start(out=group_view(xmid_rows, k), in_=xm[:])
+
+        def minus_mean(k, h):
+            sums, neg_mu = mean_tiles[k]
+            nc.vector.tensor_scalar(
+                out=neg_mu[:, h : h + 1],
+                in0=sums[:, h, 0:1],
+                scalar1=sums[:, h, 1:2],
+                scalar2=-1.0 / D,
+                op0=ALU.add,
+                op1=ALU.mult,
+            )
+
+        def variance(k, h):
+            if h == 0:
+                norm_tiles[k] = (
+                    small.tile([P, TILES], F32, name="ssq"),
+                    small.tile([P, TILES], F32, name="var_eps"),
+                    small.tile([P, TILES], F32, name="rstd"),
+                )
+            xm = xm_tiles[k]
+            neg_mu = mean_tiles[k][1]
+            ssq, var_eps, rstd = norm_tiles[k]
+            one = slice(h, h + 1)
+            squares = work.tile([P, D], BF16, name="squares")
+            nc.scalar.activation(
+                out=squares[:], in_=xm[:, h, :], func=ACT.Square, bias=neg_mu[:, one], scale=1.0, accum_out=ssq[:, one]
+            )
+
+        def reciprocal_std(k):
+            ssq, var_eps, rstd = norm_tiles[k]
+            nc.vector.tensor_scalar(out=var_eps[:], in0=ssq[:], scalar1=1.0 / D, scalar2=EPS, op0=ALU.mult, op1=ALU.add)
+            nc.gpsimd.tensor_tensor(out=rstd[:], in0=var_eps[:], in1=neg_half[:], op=ALU.pow)
+
+        def normalise(k, h):
+            if h == 0:
+                z_tiles[k] = work.tile([P, TILES, D], F32, name="z", bufs=4)
+            one = slice(h, h + 1)
+            engine = nc.gpsimd if h == 0 else nc.vector
+            engine.tensor_scalar(
+                out=z_tiles[k][:, h, :],
+                in0=xm_tiles[k][:, h, :],
+                scalar1=mean_tiles[k][1][:, one],
+                scalar2=norm_tiles[k][2][:, one],
+                op0=ALU.add,
+                op1=ALU.mult,
+            )
+
+        def transpose_z(k, h):
+            if h == 0:
+                plane_tiles[k] = work.tile([P, D_BLOCKS, GROUP], BF16, name="planes")
+            planes = plane_tiles[k]
+            z = z_tiles[k]
+            for b in range(2):
+                z_ps = ztp.tile([P, 2, GROUP], F32, tag="ztp")
+                for cc in range(2):
+                    t = 2 * b + cc
+                    for j in range(TILES):
+                        cols = z[:, j, 512 * h + t : 512 * (h + 1) : 4]
+                        nc.tensor.transpose(z_ps[:, cc, j * P : (j + 1) * P], cols, ident_f32[:])
+                for cc in range(2):
+                    c = 4 * h + 2 * b + cc
+                    gain = gb[:, 2 * b + cc, h : h + 1]
+                    shift = gb[:, 2 * b + cc, PASSES2 + h : PASSES2 + h + 1]
+                    if h == 1 and b == 1:
+                        nc.vector.tensor_scalar(
+                            out=planes[:, c, :], in0=z_ps[:, cc, :], scalar1=gain, scalar2=shift, op0=ALU.mult, op1=ALU.add
+                        )
+                    else:
+                        nc.scalar.activation(
+                            out=planes[:, c, :], in_=z_ps[:, cc, :], func=ACT.Identity, bias=shift, scale=gain
+                        )
+
+        def regroup_h(k, s):
+            if s == 0:
+                zgrp_tiles[k] = work.tile([P, PASSES2, GROUP, 4], BF16, align_bytes=64, name="z_grp")
+            nc.vector.tensor_copy(
+                out=zgrp_tiles[k][:, s, :, :].rearrange("p (c i) t -> p c t i", i=4),
+                in_=plane_tiles[k][:, 4 * s : 4 * s + 4, :].rearrange("p t (c i) -> p c t i", i=4),
+            )
+
+        def quantise_h(k):
+            z_codes = work.tile([P, PASSES2, GROUP], U32, align_bytes=64, name="z_codes", bufs=3)
+            z_scales = work.tile([P, PASSES2, GROUP], U8, align_bytes=64, name="z_scales", bufs=3)
+            nc.vector.quantize_mx(
+                out=z_codes[:].rearrange("p s r -> p (s r)").bitcast(FP8X4),
+                scales=z_scales[:].rearrange("p s r -> p (s r)"),
+                in_=zgrp_tiles[k][:].rearrange("p s r t -> p (s r t)"),
+            )
+            z_ops[k] = (z_codes, z_scales)
+
+        def second_matmul(k, h):
+            z_codes, z_scales = z_ops[k]
+            tok = slice(h * P, (h + 1) * P)
+            acc2 = accp.tile([P, F], F32, tag="acc")
+            for s in range(PASSES2):
+                nc.tensor.matmul_mx(
+                    out=acc2[:],
+                    lhsT=z_codes[:, s, tok].bitcast(FP8X4),
+                    lhsT_scale=z_scales[:, s, tok],
+                    rhs=w2_codes[:, s, :].bitcast(FP8X4),
+                    rhs_scale=w2_scales[:, s, :],
+                    start=(s == 0),
+                    stop=(s == PASSES2 - 1),
+                )
+            return acc2
+
+        def gelu(k, h, acc2):
+            if h == 0:
+                act_tiles[k] = work.tile([P, TILES, F], F32, name="act", bufs=3)
+            act = act_tiles[k]
+            nc.scalar.activation(out=act[:, h, :], in_=acc2[:], func=ACT.Gelu)
+            if h == TILES - 1:
+                nc.sync.dma_start(out=group_view(act_rows, k), in_=act[:])
+
+        for h in range(TILES):
+            transpose_h_attn(0, h)
+        quantise_h_attn(0)
+        quantise_w_out()
+        for h in range(TILES):
+            transpose_h_attn(1, h)
+        first_matmul(0, 0)
+        for h in range(TILES):
+            transpose_h_attn(2, h)
+        for k in range(GROUPS + 6):
+            if k % 2 == 0 and k // 2 + LOADS_AHEAD < LOADS:
+                load_h_attn(k // 2 + LOADS_AHEAD)
+                load_x(k // 2 + LOADS_AHEAD)
+            for h in range(TILES):
+                acc2 = second_matmul(k - 6, h) if live(k - 6) else None
+                after_k, after_h = (k, 1) if h == 0 else (k + 1, 0)
+                if live(after_k):
+                    first_matmul(after_k, after_h)
+                if live(k):
+                    add_residual(k, h, 0)
+                    if h == 1:
+                        minus_mean(k, 0)
+                    add_residual(k, h, 1)
+                if k == 0 and h == 0:
+                    quantise_h_attn(1)
+                before_k, before_h = (k - 1, 1) if h == 0 else (k, 0)
+                if live(before_k):
+                    variance(before_k, before_h)
+                if live(k - 6):
+                    gelu(k - 6, h, acc2)
+                if h == 1:
+                    if live(k - 4):
+                        regroup_h(k - 4, 0)
+                    if live(k):
+                        minus_mean(k, 1)
+                    if live(k - 4):
+                        regroup_h(k - 4, 1)
+                    if live(k + 2):
+                        quantise_h_attn(k + 2)
+                    if live(k - 2):
+                        normalise(k - 2, 1)
+                    if live(k - 4):
+                        quantise_h(k - 4)
+                    if live(k - 1):
+                        reciprocal_std(k - 1)
+                        normalise(k - 1, 0)
+                if live(k - 3):
+                    transpose_z(k - 3, h)
+                if live(k + 3):
+                    transpose_h_attn(k + 3, h)
+                if k == 1 and h == 1:
+                    transpose_gain_and_bias()
+                if k == 2 or k == 3:
+                    transpose_w_fc1(k - 2, h)
+                if k == 5:
+                    quantise_w_fc1(h)

@@ -79,12 +79,12 @@ def tile_minitransformerlayer_pb_t_kernel(tc, h_attn, x, w_out, w_fc1, g2, b2, o
         load_h_attn(1)
         load_h_attn(2)
         load_x(1)
-        gb_rows = const.tile([P, 512], BF16)
+        gb_rows = const.tile([P, PASSES2 * 256], BF16)
         nc.vector.memset(gb_rows[:], 0.0)
         nc.sync.dma_start(out=gb_rows[0:PASSES2, :], in_=g2.rearrange("(s k) -> s k", k=512))
         nc.sync.dma_start(out=gb_rows[PASSES2 : 2 * PASSES2, :], in_=b2.rearrange("(s k) -> s k", k=512))
-        w2_raw = const.tile([P, F // P, D], BF16)
-        nc.sync.dma_start(out=w2_raw[:], in_=w_fc1.rearrange("(r p) k -> p r k", p=P))
+        w2_raw = const.tile([P, F // P * D], BF16)
+        nc.sync.dma_start(out=w2_raw[:].rearrange("p (r k) -> p r k", k=D), in_=w_fc1.rearrange("(r p) k -> p r k", p=P))
         load_x(2)
 
         ident_f32 = const.tile([P, P], F32)
@@ -126,10 +126,23 @@ def tile_minitransformerlayer_pb_t_kernel(tc, h_attn, x, w_out, w_fc1, g2, b2, o
         gb = const.tile([P, 4, 2 * PASSES2], F32)
 
         def transpose_gain_and_bias():
+            gb_perm = const.tile([P, 4, P], BF16)
+            nc.vector.tensor_copy(
+                out=gb_perm[:].rearrange("p t (q r) -> p t q r", r=8),
+                in_=gb_rows[:].rearrange("p (q t r) -> p t q r", t=4, r=8),
+            )
             gb_ps = ztp.tile([P, 4, P], BF16, tag="ztp")
             for t in range(4):
-                nc.tensor.transpose(gb_ps[:, t, :], gb_rows[:, t:512:4], ident_bf[:])
+                nc.tensor.transpose(gb_ps[:, t, :], gb_perm[:, t, :], ident_bf[:])
             nc.scalar.copy(out=gb[:], in_=gb_ps[:, :, 0 : 2 * PASSES2])
+
+        w2_perm = const.tile([P, 4, F // P, PASSES2, P], BF16)
+
+        def permute_w_fc1():
+            nc.vector.tensor_copy(
+                out=w2_perm[:].rearrange("p t f s (q r) -> p t (f s q) r", r=8),
+                in_=w2_raw[:].rearrange("p (g t r) -> p t g r", t=4, r=8),
+            )
 
         w2_grp = const.tile([P, PASSES2, F, 4], BF16, align_bytes=64)
         w2_codes = const.tile([P, PASSES2, F], U32, align_bytes=64)
@@ -139,9 +152,7 @@ def tile_minitransformerlayer_pb_t_kernel(tc, h_attn, x, w_out, w_fc1, g2, b2, o
             w2_ps = ztp.tile([P, 4, 2 * P], BF16, tag="ztp")
             for t in range(4):
                 for rr in range(2):
-                    nc.tensor.transpose(
-                        w2_ps[:, t, rr * P : (rr + 1) * P], w2_raw[:, 2 * q + rr, 512 * s + t : 512 * (s + 1) : 4], ident_bf[:]
-                    )
+                    nc.tensor.transpose(w2_ps[:, t, rr * P : (rr + 1) * P], w2_perm[:, t, 2 * q + rr, s, :], ident_bf[:])
             nc.scalar.copy(out=w2_grp[:, s, q * 2 * P : (q + 1) * 2 * P, :], in_=w2_ps[:].rearrange("p t f -> p f t"))
 
         def quantise_w_fc1(s):
@@ -263,12 +274,12 @@ def tile_minitransformerlayer_pb_t_kernel(tc, h_attn, x, w_out, w_fc1, g2, b2, o
 
         def normalise(k, h):
             if h == 0:
-                z_tiles[k] = work.tile([P, TILES, D], F32, name="z", bufs=4)
+                z_tiles[k] = work.tile([P, TILES, 4, D // 4], F32, name="z", bufs=4)
             one = slice(h, h + 1)
             engine = nc.gpsimd if h == 0 else nc.vector
             engine.tensor_scalar(
-                out=z_tiles[k][:, h, :],
-                in0=xm_tiles[k][:, h, :],
+                out=z_tiles[k][:, h, :, :].rearrange("p t (g r) -> p t g r", r=8),
+                in0=xm_tiles[k][:, h, :].rearrange("p (g t r) -> p t g r", t=4, r=8),
                 scalar1=mean_tiles[k][1][:, one],
                 scalar2=norm_tiles[k][2][:, one],
                 op0=ALU.add,
@@ -285,8 +296,7 @@ def tile_minitransformerlayer_pb_t_kernel(tc, h_attn, x, w_out, w_fc1, g2, b2, o
                 for cc in range(2):
                     t = 2 * b + cc
                     for j in range(TILES):
-                        cols = z[:, j, 512 * h + t : 512 * (h + 1) : 4]
-                        nc.tensor.transpose(z_ps[:, cc, j * P : (j + 1) * P], cols, ident_f32[:])
+                        nc.tensor.transpose(z_ps[:, cc, j * P : (j + 1) * P], z[:, j, t, h * P : (h + 1) * P], ident_f32[:])
                 for cc in range(2):
                     c = 4 * h + 2 * b + cc
                     gain = gb[:, 2 * b + cc, h : h + 1]
@@ -394,6 +404,8 @@ def tile_minitransformerlayer_pb_t_kernel(tc, h_attn, x, w_out, w_fc1, g2, b2, o
                     transpose_h_attn(k + 3, h)
                 if k == 1 and h == 1:
                     transpose_gain_and_bias()
+                if k == 1 and h == 1:
+                    permute_w_fc1()
                 if k == 2 or k == 3:
                     transpose_w_fc1(k - 2, h)
                 if k == 5:

@@ -20,12 +20,14 @@ EPS = 1e-5
 BANK = 512
 D_BLOCKS = D // P
 PASSES2 = D // 512
+RUN = 8
 LOAD_TILES = 4
 LOAD_TOKENS = LOAD_TILES * P
 LOADS = TOKENS // LOAD_TOKENS
 TILES = 2
 GROUP = TILES * P
 GROUPS = TOKENS // GROUP
+LAST = GROUPS - 1
 LOADS_AHEAD = 3
 
 FLOPS = 2 * TOKENS * E * D + 2 * TOKENS * D * F
@@ -51,40 +53,48 @@ def tile_minitransformerlayer_pb_t_kernel(tc, h_attn, x, w_out, w_fc1, g2, b2, o
         def load_view(rows, n):
             return rows[n * LOAD_TOKENS : (n + 1) * LOAD_TOKENS, :].rearrange("(p j) c -> p j c", j=LOAD_TILES)
 
-        def group_view(rows, k):
+        def group_tiles(k):
             first = (k % 2) * TILES
-            return load_view(rows, k // 2)[:, first : first + TILES, :]
+            return slice(first, first + TILES)
+
+        def group_view(rows, k):
+            return load_view(rows, k // 2)[:, group_tiles(k), :]
 
         ha_tiles = {}
         x_tiles = {}
 
         def load_h_attn(n):
-            ha_sb = loads.tile([P, LOAD_TILES * E], BF16, name="ha_sb")
-            nc.sync.dma_start(out=ha_sb[:].rearrange("p (j c) -> p j c", j=LOAD_TILES), in_=load_view(ha_rows, n))
-            ha_tiles[n] = ha_sb
+            ha_tiles[n] = loads.tile([P, LOAD_TILES, E], BF16, name="ha_sb")
+            nc.sync.dma_start(out=ha_tiles[n][:], in_=load_view(ha_rows, n))
 
         def load_x(n):
-            x_sb = loads.tile([P, LOAD_TILES, D], BF16, name="x_sb")
-            nc.sync.dma_start(out=x_sb[:], in_=load_view(x_rows, n))
-            x_tiles[n] = x_sb
+            x_tiles[n] = loads.tile([P, LOAD_TILES, D], BF16, name="x_sb")
+            nc.sync.dma_start(out=x_tiles[n][:], in_=load_view(x_rows, n))
 
-        load_h_attn(0)
-        w1_raw = const.tile([P, D_BLOCKS * E], BF16)
-        w1_raw_blocks = w1_raw[:].rearrange("p (r k) -> p r k", k=E)
+        w1_raw = const.tile([P, D_BLOCKS, E], BF16)
         w_out_blocks = w_out.rearrange("(r p) k -> p r k", p=P)
-        for half in range(D // BANK):
-            blocks = slice(half * BANK // P, (half + 1) * BANK // P)
-            nc.sync.dma_start(out=w1_raw_blocks[:, blocks, :], in_=w_out_blocks[:, blocks, :])
-        load_x(0)
-        load_h_attn(1)
-        load_h_attn(2)
-        load_x(1)
+        w2_raw = const.tile([P, F // P * D], BF16)
         gb_rows = const.tile([P, PASSES2 * 256], BF16)
         nc.vector.memset(gb_rows[:], 0.0)
+        ha_tiles[0] = loads.tile([P, LOAD_TILES, E], BF16, name="ha_sb")
+        x_tiles[0] = loads.tile([P, LOAD_TILES, D], BF16, name="x_sb")
+
+        def load_first(tile, rows, k):
+            nc.sync.dma_start(out=tile[:, group_tiles(k), :], in_=group_view(rows, k))
+
+        load_first(ha_tiles[0], ha_rows, 0)
+        for q in range(D_BLOCKS // 2):
+            two = slice(2 * q, 2 * q + 2)
+            nc.sync.dma_start(out=w1_raw[:, two, :], in_=w_out_blocks[:, two, :])
+        load_first(x_tiles[0], x_rows, 0)
+        load_first(ha_tiles[0], ha_rows, 1)
+        load_first(x_tiles[0], x_rows, 1)
+        load_h_attn(1)
+        nc.sync.dma_start(out=w2_raw[:].rearrange("p (r k) -> p r k", k=D), in_=w_fc1.rearrange("(r p) k -> p r k", p=P))
+        load_x(1)
         nc.sync.dma_start(out=gb_rows[0:PASSES2, :], in_=g2.rearrange("(s k) -> s k", k=512))
         nc.sync.dma_start(out=gb_rows[PASSES2 : 2 * PASSES2, :], in_=b2.rearrange("(s k) -> s k", k=512))
-        w2_raw = const.tile([P, F // P * D], BF16)
-        nc.sync.dma_start(out=w2_raw[:].rearrange("p (r k) -> p r k", k=D), in_=w_fc1.rearrange("(r p) k -> p r k", p=P))
+        load_h_attn(2)
         load_x(2)
 
         ident_f32 = const.tile([P, P], F32)
@@ -99,37 +109,38 @@ def tile_minitransformerlayer_pb_t_kernel(tc, h_attn, x, w_out, w_fc1, g2, b2, o
 
         w1_grp = const.tile([P, D * 4], BF16, align_bytes=64)
         w1_grp_words = w1_grp[:].bitcast(F32).rearrange("p (d u) -> p d u", u=2)
-        w1_words = w1_raw[:].bitcast(F32)
         w1_codes = const.tile([P, D], U32, align_bytes=64)
         w1_scales = const.tile([P, D], U8, align_bytes=64)
 
-        def quantise_w_out():
-            for q in range(D_BLOCKS // 2):
-                w1_ps = ztp.tile([P, 2, 2 * P], F32, tag="ztp")
-                for rr in range(2):
-                    for u in range(2):
-                        row = 2 * q + rr
-                        words = w1_words[:, row * (E // 2) + u : (row + 1) * (E // 2) : 2]
-                        nc.tensor.transpose(w1_ps[:, u, rr * P : (rr + 1) * P], words, ident_f32[:])
-                w1_out = w1_grp_words[:, q * 2 * P : (q + 1) * 2 * P, :]
-                if q % 2 == 0:
-                    nc.vector.tensor_copy(out=w1_out, in_=w1_ps[:].rearrange("p u d -> p d u"))
-                else:
-                    nc.scalar.copy(out=w1_out, in_=w1_ps[:].rearrange("p u d -> p d u"))
-                    half = q // 2
-                    nc.vector.quantize_mx(
-                        out=w1_codes[:, half * BANK : (half + 1) * BANK].bitcast(FP8X4),
-                        scales=w1_scales[:, half * BANK : (half + 1) * BANK],
-                        in_=w1_grp[:, half * BANK * 4 : (half + 1) * BANK * 4],
-                    )
+        def transpose_w_out(q):
+            w1_words = w1_raw[:].rearrange("p r k -> p (r k)").bitcast(F32)
+            pool, tag = (ztp, "ztp") if q < 2 else (accp, "acc")
+            w1_ps = pool.tile([P, 2, 2 * P], F32, tag=tag, name="w1_ps")
+            for rr in range(2):
+                for u in range(2):
+                    row = 2 * q + rr
+                    words = w1_words[:, row * (E // 2) + u : (row + 1) * (E // 2) : 2]
+                    nc.tensor.transpose(w1_ps[:, u, rr * P : (rr + 1) * P], words, ident_f32[:])
+            w1_out = w1_grp_words[:, q * 2 * P : (q + 1) * 2 * P, :]
+            if q % 2 == 0:
+                nc.vector.tensor_copy(out=w1_out, in_=w1_ps[:].rearrange("p u d -> p d u"))
+            else:
+                nc.scalar.copy(out=w1_out, in_=w1_ps[:].rearrange("p u d -> p d u"))
+
+        def quantise_w_out(half):
+            nc.vector.quantize_mx(
+                out=w1_codes[:, half * BANK : (half + 1) * BANK].bitcast(FP8X4),
+                scales=w1_scales[:, half * BANK : (half + 1) * BANK],
+                in_=w1_grp[:, half * BANK * 4 : (half + 1) * BANK * 4],
+            )
 
         gb = const.tile([P, 4, 2 * PASSES2], F32)
 
         def transpose_gain_and_bias():
             gb_perm = const.tile([P, 4, P], BF16)
             nc.vector.tensor_copy(
-                out=gb_perm[:].rearrange("p t (q r) -> p t q r", r=8),
-                in_=gb_rows[:].rearrange("p (q t r) -> p t q r", t=4, r=8),
+                out=gb_perm[:].rearrange("p t (q r) -> p t q r", r=RUN),
+                in_=gb_rows[:].rearrange("p (q t r) -> p t q r", t=4, r=RUN),
             )
             gb_ps = ztp.tile([P, 4, P], BF16, tag="ztp")
             for t in range(4):
@@ -137,23 +148,26 @@ def tile_minitransformerlayer_pb_t_kernel(tc, h_attn, x, w_out, w_fc1, g2, b2, o
             nc.scalar.copy(out=gb[:], in_=gb_ps[:, :, 0 : 2 * PASSES2])
 
         w2_perm = const.tile([P, 4, F // P, PASSES2, P], BF16)
-
-        def permute_w_fc1():
-            nc.vector.tensor_copy(
-                out=w2_perm[:].rearrange("p t f s (q r) -> p t (f s q) r", r=8),
-                in_=w2_raw[:].rearrange("p (g t r) -> p t g r", t=4, r=8),
-            )
-
         w2_grp = const.tile([P, PASSES2, F, 4], BF16, align_bytes=64)
         w2_codes = const.tile([P, PASSES2, F], U32, align_bytes=64)
         w2_scales = const.tile([P, PASSES2, F], U8, align_bytes=64)
+
+        def permute_w_fc1():
+            nc.vector.tensor_copy(
+                out=w2_perm[:].rearrange("p t f s (q r) -> p t (f s q) r", r=RUN),
+                in_=w2_raw[:].rearrange("p (g t r) -> p t g r", t=4, r=RUN),
+            )
 
         def transpose_w_fc1(s, q):
             w2_ps = ztp.tile([P, 4, 2 * P], BF16, tag="ztp")
             for t in range(4):
                 for rr in range(2):
                     nc.tensor.transpose(w2_ps[:, t, rr * P : (rr + 1) * P], w2_perm[:, t, 2 * q + rr, s, :], ident_bf[:])
-            nc.scalar.copy(out=w2_grp[:, s, q * 2 * P : (q + 1) * 2 * P, :], in_=w2_ps[:].rearrange("p t f -> p f t"))
+            w2_out = w2_grp[:, s, q * 2 * P : (q + 1) * 2 * P, :]
+            if q == 0:
+                nc.vector.tensor_copy(out=w2_out, in_=w2_ps[:].rearrange("p t f -> p f t"))
+            else:
+                nc.scalar.copy(out=w2_out, in_=w2_ps[:].rearrange("p t f -> p f t"))
 
         def quantise_w_fc1(s):
             nc.vector.quantize_mx(
@@ -169,6 +183,7 @@ def tile_minitransformerlayer_pb_t_kernel(tc, h_attn, x, w_out, w_fc1, g2, b2, o
         xm_tiles = {}
         mean_tiles = {}
         z_tiles = {}
+        z_banks = {}
         norm_tiles = {}
         plane_tiles = {}
         zgrp_tiles = {}
@@ -178,21 +193,21 @@ def tile_minitransformerlayer_pb_t_kernel(tc, h_attn, x, w_out, w_fc1, g2, b2, o
         def live(k):
             return 0 <= k < GROUPS
 
-        def transpose_h_attn(k, h):
-            if h == 0:
-                h_banks[k] = htp.tile([P, 2, GROUP], F32, name="h_ps")
-            h_ps = h_banks[k]
-            ha_words = ha_tiles[k // 2][:].bitcast(F32)
-            for u in range(2):
-                row = (k % 2) * TILES + h
-                words = ha_words[:, row * (E // 2) + u : (row + 1) * (E // 2) : 2]
-                nc.tensor.transpose(h_ps[:, u, h * P : (h + 1) * P], words, ident_f32[:])
-            if h == TILES - 1:
-                h_grp = work.tile([P, GROUP * 4], BF16, align_bytes=64, name="h_grp", bufs=3)
-                nc.scalar.copy(
-                    out=h_grp[:].bitcast(F32).rearrange("p (r u) -> p r u", u=2), in_=h_ps[:].rearrange("p u r -> p r u")
-                )
-                h_groups[k] = h_grp
+        def transpose_h_attn(k):
+            h_banks[k] = htp.tile([P, 2, GROUP], F32, name="h_ps")
+            ha_words = ha_tiles[k // 2][:].rearrange("p j c -> p (j c)").bitcast(F32)
+            for h in range(TILES):
+                for u in range(2):
+                    row = (k % 2) * TILES + h
+                    words = ha_words[:, row * (E // 2) + u : (row + 1) * (E // 2) : 2]
+                    nc.tensor.transpose(h_banks[k][:, u, h * P : (h + 1) * P], words, ident_f32[:])
+
+        def copy_h_attn(k):
+            h_groups[k] = work.tile([P, GROUP * 4], BF16, align_bytes=64, name="h_grp", bufs=3)
+            nc.scalar.copy(
+                out=h_groups[k][:].bitcast(F32).rearrange("p (r u) -> p r u", u=2),
+                in_=h_banks[k][:].rearrange("p u r -> p r u"),
+            )
 
         def quantise_h_attn(k):
             h_codes = work.tile([P, GROUP], U32, align_bytes=64, name="h_codes", bufs=4)
@@ -200,45 +215,46 @@ def tile_minitransformerlayer_pb_t_kernel(tc, h_attn, x, w_out, w_fc1, g2, b2, o
             nc.vector.quantize_mx(out=h_codes[:].bitcast(FP8X4), scales=h_scales[:], in_=h_groups[k][:])
             h_ops[k] = (h_codes, h_scales)
 
-        def first_matmul(k, h):
+        def first_matmul(k, h, half):
             h_codes, h_scales = h_ops[k]
             tok = slice(h * P, (h + 1) * P)
-            for half in range(D // BANK):
-                cols = slice(half * BANK, (half + 1) * BANK)
-                acc1 = accp.tile([P, BANK], F32, tag="acc")
-                nc.tensor.matmul_mx(
-                    out=acc1[:],
-                    lhsT=h_codes[:, tok].bitcast(FP8X4),
-                    lhsT_scale=h_scales[:, tok],
-                    rhs=w1_codes[:, cols].bitcast(FP8X4),
-                    rhs_scale=w1_scales[:, cols],
-                    start=True,
-                    stop=True,
-                )
-                acc1_banks[(k, h, half)] = acc1
+            cols = slice(half * BANK, (half + 1) * BANK)
+            acc1 = accp.tile([P, BANK], F32, tag="acc")
+            nc.tensor.matmul_mx(
+                out=acc1[:],
+                lhsT=h_codes[:, tok].bitcast(FP8X4),
+                lhsT_scale=h_scales[:, tok],
+                rhs=w1_codes[:, cols].bitcast(FP8X4),
+                rhs_scale=w1_scales[:, cols],
+                start=True,
+                stop=True,
+            )
+            acc1_banks[(k, h, half)] = acc1
+
+        def start_group(k):
+            xm_tiles[k] = work.tile([P, TILES, D], F32, name="xm", bufs=4)
+            mean_tiles[k] = (small.tile([P, TILES, 2], F32, name="sums"), small.tile([P, TILES], F32, name="neg_mu"))
+            norm_tiles[k] = (
+                small.tile([P, TILES], F32, name="ssq"),
+                small.tile([P, TILES], F32, name="var_eps"),
+                small.tile([P, TILES], F32, name="rstd"),
+            )
+            z_tiles[k] = work.tile([P, TILES, 4, D // 4], F32, name="z", bufs=3)
 
         def add_residual(k, h, half):
-            if h == 0 and half == 0:
-                xm_tiles[k] = work.tile([P, TILES, D], F32, name="xm", bufs=4)
-                mean_tiles[k] = (
-                    small.tile([P, TILES, 2], F32, name="sums"),
-                    small.tile([P, TILES], F32, name="neg_mu"),
-                )
-            xm = xm_tiles[k]
-            sums = mean_tiles[k][0]
-            x_sb = x_tiles[k // 2]
             cols = slice(half * BANK, (half + 1) * BANK)
             nc.vector.scalar_tensor_tensor(
-                out=xm[:, h, cols],
+                out=xm_tiles[k][:, h, cols],
                 in0=acc1_banks[(k, h, half)][:],
                 scalar=1.0,
-                in1=x_sb[:, (k % 2) * TILES + h, cols],
+                in1=x_tiles[k // 2][:, (k % 2) * TILES + h, cols],
                 op0=ALU.mult,
                 op1=ALU.add,
-                accum_out=sums[:, h, half : half + 1],
+                accum_out=mean_tiles[k][0][:, h, half : half + 1],
             )
-            if h == TILES - 1 and half == 1:
-                nc.sync.dma_start(out=group_view(xmid_rows, k), in_=xm[:])
+
+        def store_xmid(k):
+            nc.sync.dma_start(out=group_view(xmid_rows, k), in_=xm_tiles[k][:])
 
         def minus_mean(k, h):
             sums, neg_mu = mean_tiles[k]
@@ -252,19 +268,15 @@ def tile_minitransformerlayer_pb_t_kernel(tc, h_attn, x, w_out, w_fc1, g2, b2, o
             )
 
         def variance(k, h):
-            if h == 0:
-                norm_tiles[k] = (
-                    small.tile([P, TILES], F32, name="ssq"),
-                    small.tile([P, TILES], F32, name="var_eps"),
-                    small.tile([P, TILES], F32, name="rstd"),
-                )
-            xm = xm_tiles[k]
-            neg_mu = mean_tiles[k][1]
-            ssq, var_eps, rstd = norm_tiles[k]
             one = slice(h, h + 1)
             squares = work.tile([P, D], BF16, name="squares")
             nc.scalar.activation(
-                out=squares[:], in_=xm[:, h, :], func=ACT.Square, bias=neg_mu[:, one], scale=1.0, accum_out=ssq[:, one]
+                out=squares[:],
+                in_=xm_tiles[k][:, h, :],
+                func=ACT.Square,
+                bias=mean_tiles[k][1][:, one],
+                scale=1.0,
+                accum_out=norm_tiles[k][0][:, one],
             )
 
         def reciprocal_std(k):
@@ -272,43 +284,41 @@ def tile_minitransformerlayer_pb_t_kernel(tc, h_attn, x, w_out, w_fc1, g2, b2, o
             nc.vector.tensor_scalar(out=var_eps[:], in0=ssq[:], scalar1=1.0 / D, scalar2=EPS, op0=ALU.mult, op1=ALU.add)
             nc.gpsimd.tensor_tensor(out=rstd[:], in0=var_eps[:], in1=neg_half[:], op=ALU.pow)
 
-        def normalise(k, h):
-            if h == 0:
-                z_tiles[k] = work.tile([P, TILES, 4, D // 4], F32, name="z", bufs=4)
+        def normalise(engine, k, h, blocks):
             one = slice(h, h + 1)
-            engine = nc.gpsimd if h == 0 else nc.vector
             engine.tensor_scalar(
-                out=z_tiles[k][:, h, :, :].rearrange("p t (g r) -> p t g r", r=8),
-                in0=xm_tiles[k][:, h, :].rearrange("p (g t r) -> p t g r", t=4, r=8),
+                out=z_tiles[k][:, h, blocks, :].rearrange("p t (g r) -> p t g r", r=RUN),
+                in0=xm_tiles[k][:, h, :].rearrange("p (g t r) -> p t g r", t=4, r=RUN)[:, blocks, :, :],
                 scalar1=mean_tiles[k][1][:, one],
                 scalar2=norm_tiles[k][2][:, one],
                 op0=ALU.add,
                 op1=ALU.mult,
             )
 
-        def transpose_z(k, h):
-            if h == 0:
+        def transpose_z(k, s, b):
+            pool, tag = (accp, "acc") if k == LAST and s == 1 else (ztp, "ztp")
+            z_ps = pool.tile([P, 2, GROUP], F32, tag=tag, name="z_ps")
+            for cc in range(2):
+                for j in range(TILES):
+                    nc.tensor.transpose(
+                        z_ps[:, cc, j * P : (j + 1) * P], z_tiles[k][:, j, 2 * b + cc, s * P : (s + 1) * P], ident_f32[:]
+                    )
+            z_banks[(k, s, b)] = z_ps
+
+        def empty_z(k, s, b):
+            if s == 0 and b == 0:
                 plane_tiles[k] = work.tile([P, D_BLOCKS, GROUP], BF16, name="planes")
-            planes = plane_tiles[k]
-            z = z_tiles[k]
-            for b in range(2):
-                z_ps = ztp.tile([P, 2, GROUP], F32, tag="ztp")
-                for cc in range(2):
-                    t = 2 * b + cc
-                    for j in range(TILES):
-                        nc.tensor.transpose(z_ps[:, cc, j * P : (j + 1) * P], z[:, j, t, h * P : (h + 1) * P], ident_f32[:])
-                for cc in range(2):
-                    c = 4 * h + 2 * b + cc
-                    gain = gb[:, 2 * b + cc, h : h + 1]
-                    shift = gb[:, 2 * b + cc, PASSES2 + h : PASSES2 + h + 1]
-                    if h == 1 and b == 1:
-                        nc.vector.tensor_scalar(
-                            out=planes[:, c, :], in0=z_ps[:, cc, :], scalar1=gain, scalar2=shift, op0=ALU.mult, op1=ALU.add
-                        )
-                    else:
-                        nc.scalar.activation(
-                            out=planes[:, c, :], in_=z_ps[:, cc, :], func=ACT.Identity, bias=shift, scale=gain
-                        )
+            on_vector = b == 1 and s == 1
+            for cc in range(2):
+                t = 2 * b + cc
+                plane = plane_tiles[k][:, 4 * s + t, :]
+                bank = z_banks[(k, s, b)][:, cc, :]
+                gain = gb[:, t, s : s + 1]
+                shift = gb[:, t, PASSES2 + s : PASSES2 + s + 1]
+                if on_vector:
+                    nc.vector.tensor_scalar(out=plane, in0=bank, scalar1=gain, scalar2=shift, op0=ALU.mult, op1=ALU.add)
+                else:
+                    nc.scalar.activation(out=plane, in_=bank, func=ACT.Identity, bias=shift, scale=gain)
 
         def regroup_h(k, s):
             if s == 0:
@@ -328,13 +338,15 @@ def tile_minitransformerlayer_pb_t_kernel(tc, h_attn, x, w_out, w_fc1, g2, b2, o
             )
             z_ops[k] = (z_codes, z_scales)
 
+        acc2_banks = {}
+
         def second_matmul(k, h):
             z_codes, z_scales = z_ops[k]
             tok = slice(h * P, (h + 1) * P)
-            acc2 = accp.tile([P, F], F32, tag="acc")
+            acc2_banks[(k, h)] = accp.tile([P, F], F32, tag="acc", name="acc2")
             for s in range(PASSES2):
                 nc.tensor.matmul_mx(
-                    out=acc2[:],
+                    out=acc2_banks[(k, h)][:],
                     lhsT=z_codes[:, s, tok].bitcast(FP8X4),
                     lhsT_scale=z_scales[:, s, tok],
                     rhs=w2_codes[:, s, :].bitcast(FP8X4),
@@ -342,71 +354,160 @@ def tile_minitransformerlayer_pb_t_kernel(tc, h_attn, x, w_out, w_fc1, g2, b2, o
                     start=(s == 0),
                     stop=(s == PASSES2 - 1),
                 )
-            return acc2
 
-        def gelu(k, h, acc2):
+        def gelu(k, h):
             if h == 0:
                 act_tiles[k] = work.tile([P, TILES, F], F32, name="act", bufs=3)
-            act = act_tiles[k]
-            nc.scalar.activation(out=act[:, h, :], in_=acc2[:], func=ACT.Gelu)
-            if h == TILES - 1:
-                nc.sync.dma_start(out=group_view(act_rows, k), in_=act[:])
+            nc.scalar.activation(out=act_tiles[k][:, h, :], in_=acc2_banks[(k, h)][:], func=ACT.Gelu)
+            if k == LAST:
+                j = (k % 2) * TILES + h
+                nc.sync.dma_start(out=load_view(act_rows, k // 2)[:, j, :], in_=act_tiles[k][:, h, :])
+            elif h == TILES - 1:
+                nc.sync.dma_start(out=group_view(act_rows, k), in_=act_tiles[k][:])
 
-        for h in range(TILES):
-            transpose_h_attn(0, h)
+        transpose_h_attn(0)
+        copy_h_attn(0)
+        transpose_w_out(0)
+        transpose_w_out(1)
         quantise_h_attn(0)
-        quantise_w_out()
+        transpose_w_out(2)
+        transpose_w_out(3)
+        quantise_w_out(0)
         for h in range(TILES):
-            transpose_h_attn(1, h)
-        first_matmul(0, 0)
+            first_matmul(0, h, 0)
+        transpose_h_attn(1)
+        copy_h_attn(1)
+        quantise_w_out(1)
         for h in range(TILES):
-            transpose_h_attn(2, h)
-        for k in range(GROUPS + 6):
+            first_matmul(0, h, 1)
+
+        def normalise_on_gpsimd(k):
+            reciprocal_std(k)
+            normalise(nc.gpsimd, k, 0, slice(0, 4))
+            normalise(nc.gpsimd, k, 1, slice(0, 2))
+
+        for k in range(GROUPS):
+            z = k - 1
+            r = k - 2
+            m = k - 3
             if k % 2 == 0 and k // 2 + LOADS_AHEAD < LOADS:
                 load_h_attn(k // 2 + LOADS_AHEAD)
                 load_x(k // 2 + LOADS_AHEAD)
-            for h in range(TILES):
-                acc2 = second_matmul(k - 6, h) if live(k - 6) else None
-                after_k, after_h = (k, 1) if h == 0 else (k + 1, 0)
-                if live(after_k):
-                    first_matmul(after_k, after_h)
-                if live(k):
-                    add_residual(k, h, 0)
-                    if h == 1:
-                        minus_mean(k, 0)
-                    add_residual(k, h, 1)
-                if k == 0 and h == 0:
-                    quantise_h_attn(1)
-                before_k, before_h = (k - 1, 1) if h == 0 else (k, 0)
-                if live(before_k):
-                    variance(before_k, before_h)
-                if live(k - 6):
-                    gelu(k - 6, h, acc2)
-                if h == 1:
-                    if live(k - 4):
-                        regroup_h(k - 4, 0)
-                    if live(k):
-                        minus_mean(k, 1)
-                    if live(k - 4):
-                        regroup_h(k - 4, 1)
-                    if live(k + 2):
-                        quantise_h_attn(k + 2)
-                    if live(k - 2):
-                        normalise(k - 2, 1)
-                    if live(k - 4):
-                        quantise_h(k - 4)
-                    if live(k - 1):
-                        reciprocal_std(k - 1)
-                        normalise(k - 1, 0)
-                if live(k - 3):
-                    transpose_z(k - 3, h)
-                if live(k + 3):
-                    transpose_h_attn(k + 3, h)
-                if k == 1 and h == 1:
-                    transpose_gain_and_bias()
-                if k == 1 and h == 1:
+
+            start_group(k)
+            if z > 0:
+                normalise_on_gpsimd(z)
+            if r >= 0:
+                empty_z(r, 1, 0)
+            if k > 1 and live(k + 2):
+                copy_h_attn(k + 2)
+            if k == 0:
+                for half in range(2):
+                    for h in range(TILES):
+                        add_residual(k, h, half)
+                    if half == 0:
+                        quantise_h_attn(1)
+                minus_mean(k, 0)
+            else:
+                add_residual(k, 0, 0)
+                if m >= 0:
+                    second_matmul(m, 0)
+                add_residual(k, 0, 1)
+                if m >= 0:
+                    second_matmul(m, 1)
+                if k == 1:
                     permute_w_fc1()
-                if k == 2 or k == 3:
-                    transpose_w_fc1(k - 2, h)
-                if k == 5:
-                    quantise_w_fc1(h)
+                    quantise_h_attn(2)
+                    for q in range(2):
+                        transpose_w_fc1(0, q)
+                    transpose_h_attn(3)
+                    copy_h_attn(3)
+                add_residual(k, 1, 0)
+                minus_mean(k, 0)
+                if k == LAST:
+                    variance(k, 0)
+                elif m >= 0:
+                    gelu(m, 0)
+                    gelu(m, 1)
+                if k < LAST:
+                    first_matmul(k + 1, 0, 0)
+                    first_matmul(k + 1, 0, 1)
+                add_residual(k, 1, 1)
+            store_xmid(k)
+            if k == 1:
+                normalise_on_gpsimd(0)
+            if r >= 0:
+                empty_z(r, 1, 1)
+            minus_mean(k, 1)
+            if k < LAST:
+                variance(k, 0)
+            variance(k, 1)
+            if k == LAST:
+                gelu(m, 0)
+                gelu(m, 1)
+            if k == 0:
+                first_matmul(k + 1, 0, 0)
+                first_matmul(k + 1, 0, 1)
+            if k < LAST:
+                first_matmul(k + 1, 1, 0)
+                first_matmul(k + 1, 1, 1)
+            if k == 0:
+                transpose_h_attn(2)
+                copy_h_attn(2)
+            if k > 0 and live(k + 3):
+                transpose_h_attn(k + 3)
+            if k == 1:
+                for q in range(2):
+                    transpose_w_fc1(1, q)
+                transpose_gain_and_bias()
+
+            if r >= 0:
+                regroup_h(r, 0)
+            if z >= 0:
+                normalise(nc.vector, z, 1, slice(2, 4))
+            if r >= 0:
+                regroup_h(r, 1)
+            if k > 0 and live(k + 2):
+                quantise_h_attn(k + 2)
+            if k == LAST:
+                reciprocal_std(k)
+            if r >= 0:
+                quantise_h(r)
+            if k == 1:
+                quantise_w_fc1(0)
+                quantise_w_fc1(1)
+            if z >= 0:
+                for b in range(2):
+                    transpose_z(z, 0, b)
+                for b in range(2):
+                    empty_z(z, 0, b)
+                for b in range(2):
+                    transpose_z(z, 1, b)
+
+        empty_z(LAST - 1, 1, 0)
+        empty_z(LAST - 1, 1, 1)
+        for h in range(TILES):
+            second_matmul(LAST - 2, h)
+            gelu(LAST - 2, h)
+        for h in range(TILES):
+            normalise(nc.vector, LAST, h, slice(0, 4))
+        for s in range(PASSES2):
+            regroup_h(LAST - 1, s)
+        quantise_h(LAST - 1)
+        for b in range(2):
+            transpose_z(LAST, 0, b)
+        for b in range(2):
+            transpose_z(LAST, 1, b)
+        for b in range(2):
+            empty_z(LAST, 0, b)
+        for b in range(2):
+            empty_z(LAST, 1, b)
+        for h in range(TILES):
+            second_matmul(LAST - 1, h)
+            gelu(LAST - 1, h)
+        for s in range(PASSES2):
+            regroup_h(LAST, s)
+        quantise_h(LAST)
+        for h in range(TILES):
+            second_matmul(LAST, h)
+            gelu(LAST, h)

@@ -164,10 +164,7 @@ def tile_minitransformerlayer_pb_t_kernel(tc, h_attn, x, w_out, w_fc1, g2, b2, o
                 for rr in range(2):
                     nc.tensor.transpose(w2_ps[:, t, rr * P : (rr + 1) * P], w2_perm[:, t, 2 * q + rr, s, :], ident_bf[:])
             w2_out = w2_grp[:, s, q * 2 * P : (q + 1) * 2 * P, :]
-            if q == 0:
-                nc.vector.tensor_copy(out=w2_out, in_=w2_ps[:].rearrange("p t f -> p f t"))
-            else:
-                nc.scalar.copy(out=w2_out, in_=w2_ps[:].rearrange("p t f -> p f t"))
+            nc.scalar.copy(out=w2_out, in_=w2_ps[:].rearrange("p t f -> p f t"))
 
         def quantise_w_fc1(s):
             nc.vector.quantize_mx(
@@ -204,10 +201,12 @@ def tile_minitransformerlayer_pb_t_kernel(tc, h_attn, x, w_out, w_fc1, g2, b2, o
 
         def copy_h_attn(k):
             h_groups[k] = work.tile([P, GROUP * 4], BF16, align_bytes=64, name="h_grp", bufs=3)
-            nc.scalar.copy(
-                out=h_groups[k][:].bitcast(F32).rearrange("p (r u) -> p r u", u=2),
-                in_=h_banks[k][:].rearrange("p u r -> p r u"),
-            )
+            out = h_groups[k][:].bitcast(F32).rearrange("p (r u) -> p r u", u=2)
+            in_ = h_banks[k][:].rearrange("p u r -> p r u")
+            if k < 3:
+                nc.scalar.copy(out=out, in_=in_)
+            else:
+                nc.vector.tensor_copy(out=out, in_=in_)
 
         def quantise_h_attn(k):
             h_codes = work.tile([P, GROUP], U32, align_bytes=64, name="h_codes", bufs=4)
@@ -232,14 +231,13 @@ def tile_minitransformerlayer_pb_t_kernel(tc, h_attn, x, w_out, w_fc1, g2, b2, o
             acc1_banks[(k, h, half)] = acc1
 
         def start_group(k):
-            xm_tiles[k] = work.tile([P, TILES, D], F32, name="xm", bufs=4)
+            xm_tiles[k] = work.tile([P, TILES, D], F32, name="xm", bufs=5)
             mean_tiles[k] = (small.tile([P, TILES, 2], F32, name="sums"), small.tile([P, TILES], F32, name="neg_mu"))
             norm_tiles[k] = (
                 small.tile([P, TILES], F32, name="ssq"),
                 small.tile([P, TILES], F32, name="var_eps"),
                 small.tile([P, TILES], F32, name="rstd"),
             )
-            z_tiles[k] = work.tile([P, TILES, 4, D // 4], F32, name="z", bufs=3)
 
         def add_residual(k, h, half):
             cols = slice(half * BANK, (half + 1) * BANK)
@@ -279,12 +277,17 @@ def tile_minitransformerlayer_pb_t_kernel(tc, h_attn, x, w_out, w_fc1, g2, b2, o
                 accum_out=norm_tiles[k][0][:, one],
             )
 
-        def reciprocal_std(k):
+        def var_plus_eps(k):
             ssq, var_eps, rstd = norm_tiles[k]
             nc.vector.tensor_scalar(out=var_eps[:], in0=ssq[:], scalar1=1.0 / D, scalar2=EPS, op0=ALU.mult, op1=ALU.add)
+
+        def reciprocal_std(k):
+            ssq, var_eps, rstd = norm_tiles[k]
             nc.gpsimd.tensor_tensor(out=rstd[:], in0=var_eps[:], in1=neg_half[:], op=ALU.pow)
 
         def normalise(engine, k, h, blocks):
+            if k not in z_tiles:
+                z_tiles[k] = work.tile([P, TILES, 4, D // 4], F32, name="z", bufs=3)
             one = slice(h, h + 1)
             engine.tensor_scalar(
                 out=z_tiles[k][:, h, blocks, :].rearrange("p t (g r) -> p t g r", r=RUN),
@@ -295,8 +298,7 @@ def tile_minitransformerlayer_pb_t_kernel(tc, h_attn, x, w_out, w_fc1, g2, b2, o
                 op1=ALU.mult,
             )
 
-        def transpose_z(k, s, b):
-            pool, tag = (accp, "acc") if k == LAST and s == 1 else (ztp, "ztp")
+        def transpose_z(k, s, b, pool=ztp, tag="ztp"):
             z_ps = pool.tile([P, 2, GROUP], F32, tag=tag, name="z_ps")
             for cc in range(2):
                 for j in range(TILES):
@@ -308,17 +310,15 @@ def tile_minitransformerlayer_pb_t_kernel(tc, h_attn, x, w_out, w_fc1, g2, b2, o
         def empty_z(k, s, b):
             if s == 0 and b == 0:
                 plane_tiles[k] = work.tile([P, D_BLOCKS, GROUP], BF16, name="planes")
-            on_vector = b == 1 and s == 1
             for cc in range(2):
                 t = 2 * b + cc
-                plane = plane_tiles[k][:, 4 * s + t, :]
-                bank = z_banks[(k, s, b)][:, cc, :]
-                gain = gb[:, t, s : s + 1]
-                shift = gb[:, t, PASSES2 + s : PASSES2 + s + 1]
-                if on_vector:
-                    nc.vector.tensor_scalar(out=plane, in0=bank, scalar1=gain, scalar2=shift, op0=ALU.mult, op1=ALU.add)
-                else:
-                    nc.scalar.activation(out=plane, in_=bank, func=ACT.Identity, bias=shift, scale=gain)
+                nc.scalar.activation(
+                    out=plane_tiles[k][:, 4 * s + t, :],
+                    in_=z_banks[(k, s, b)][:, cc, :],
+                    func=ACT.Identity,
+                    bias=gb[:, t, PASSES2 + s : PASSES2 + s + 1],
+                    scale=gb[:, t, s : s + 1],
+                )
 
         def regroup_h(k, s):
             if s == 0:
@@ -380,133 +380,125 @@ def tile_minitransformerlayer_pb_t_kernel(tc, h_attn, x, w_out, w_fc1, g2, b2, o
         quantise_w_out(1)
         for h in range(TILES):
             first_matmul(0, h, 1)
-
-        def normalise_on_gpsimd(k):
-            reciprocal_std(k)
-            normalise(nc.gpsimd, k, 0, slice(0, 4))
-            normalise(nc.gpsimd, k, 1, slice(0, 2))
+        transpose_h_attn(2)
+        copy_h_attn(2)
 
         for k in range(GROUPS):
-            z = k - 1
-            r = k - 2
-            m = k - 3
+            n = k - 3
+            z = k - 4
+            r = k - 5
+            m = k - 6
             if k % 2 == 0 and k // 2 + LOADS_AHEAD < LOADS:
                 load_h_attn(k // 2 + LOADS_AHEAD)
                 load_x(k // 2 + LOADS_AHEAD)
-
             start_group(k)
-            if z > 0:
-                normalise_on_gpsimd(z)
-            if r >= 0:
-                empty_z(r, 1, 0)
-            if k > 1 and live(k + 2):
-                copy_h_attn(k + 2)
-            if k == 0:
-                for half in range(2):
-                    for h in range(TILES):
-                        add_residual(k, h, half)
-                    if half == 0:
-                        quantise_h_attn(1)
-                minus_mean(k, 0)
-            else:
-                add_residual(k, 0, 0)
-                if m >= 0:
-                    second_matmul(m, 0)
-                add_residual(k, 0, 1)
-                if m >= 0:
-                    second_matmul(m, 1)
-                if k == 1:
-                    permute_w_fc1()
-                    quantise_h_attn(2)
-                    for q in range(2):
-                        transpose_w_fc1(0, q)
-                    transpose_h_attn(3)
-                    copy_h_attn(3)
-                add_residual(k, 1, 0)
-                minus_mean(k, 0)
-                if k == LAST:
-                    variance(k, 0)
-                elif m >= 0:
-                    gelu(m, 0)
-                    gelu(m, 1)
-                if k < LAST:
-                    first_matmul(k + 1, 0, 0)
-                    first_matmul(k + 1, 0, 1)
-                add_residual(k, 1, 1)
-            store_xmid(k)
-            if k == 1:
-                normalise_on_gpsimd(0)
-            if r >= 0:
-                empty_z(r, 1, 1)
-            minus_mean(k, 1)
-            if k < LAST:
-                variance(k, 0)
-            variance(k, 1)
-            if k == LAST:
-                gelu(m, 0)
-                gelu(m, 1)
-            if k == 0:
-                first_matmul(k + 1, 0, 0)
-                first_matmul(k + 1, 0, 1)
-            if k < LAST:
-                first_matmul(k + 1, 1, 0)
-                first_matmul(k + 1, 1, 1)
-            if k == 0:
-                transpose_h_attn(2)
-                copy_h_attn(2)
-            if k > 0 and live(k + 3):
-                transpose_h_attn(k + 3)
-            if k == 1:
-                for q in range(2):
-                    transpose_w_fc1(1, q)
-                transpose_gain_and_bias()
 
-            if r >= 0:
-                regroup_h(r, 0)
-            if z >= 0:
-                normalise(nc.vector, z, 1, slice(2, 4))
-            if r >= 0:
-                regroup_h(r, 1)
-            if k > 0 and live(k + 2):
-                quantise_h_attn(k + 2)
-            if k == LAST:
-                reciprocal_std(k)
-            if r >= 0:
-                quantise_h(r)
-            if k == 1:
-                quantise_w_fc1(0)
-                quantise_w_fc1(1)
+            if k >= 2:
+                reciprocal_std(k - 2)
+            if n >= 0:
+                normalise(nc.gpsimd, n, 0, slice(0, 4))
+                normalise(nc.gpsimd, n, 1, slice(0, 3))
+
             if z >= 0:
                 for b in range(2):
                     transpose_z(z, 0, b)
-                for b in range(2):
                     empty_z(z, 0, b)
+            if k == 0:
+                add_residual(0, 0, 0)
+                add_residual(0, 1, 0)
+            else:
+                add_residual(k, 0, 0)
+            if m >= 0:
+                second_matmul(m, 0)
+            if k == 0:
+                quantise_h_attn(1)
+                first_matmul(1, 0, 0)
+                first_matmul(1, 0, 1)
+                add_residual(0, 0, 1)
+                add_residual(0, 1, 1)
+                minus_mean(0, 0)
+                first_matmul(1, 1, 0)
+                first_matmul(1, 1, 1)
+            else:
+                add_residual(k, 0, 1)
+                add_residual(k, 1, 0)
+                minus_mean(k, 0)
+                if k < LAST:
+                    first_matmul(k + 1, 0, 0)
+                    first_matmul(k + 1, 0, 1)
+            variance(k, 0)
+            if m >= 0:
+                gelu(m, 0)
+            if k > 0:
+                add_residual(k, 1, 1)
+            store_xmid(k)
+            if k > 0 and live(k + 2):
+                copy_h_attn(k + 2)
+            minus_mean(k, 1)
+            variance(k, 1)
+            if z >= 0:
                 for b in range(2):
                     transpose_z(z, 1, b)
+                    empty_z(z, 1, b)
+            if m >= 0:
+                second_matmul(m, 1)
+            if 0 < k < LAST:
+                first_matmul(k + 1, 1, 0)
+                first_matmul(k + 1, 1, 1)
+            if live(k + 3):
+                transpose_h_attn(k + 3)
+            if m >= 0:
+                gelu(m, 1)
 
-        empty_z(LAST - 1, 1, 0)
-        empty_z(LAST - 1, 1, 1)
-        for h in range(TILES):
-            second_matmul(LAST - 2, h)
-            gelu(LAST - 2, h)
-        for h in range(TILES):
-            normalise(nc.vector, LAST, h, slice(0, 4))
+            if n >= 0:
+                normalise(nc.vector, n, 1, slice(3, 4))
+            if r >= 0:
+                regroup_h(r, 0)
+                regroup_h(r, 1)
+            if live(k + 2):
+                quantise_h_attn(k + 2)
+            if r >= 0:
+                quantise_h(r)
+            if k >= 1:
+                var_plus_eps(k - 1)
+            if k == 0:
+                permute_w_fc1()
+            if k == 1 or k == 2:
+                for q in range(2):
+                    transpose_w_fc1(k - 1, q)
+            if k == 1:
+                transpose_gain_and_bias()
+            if k == 3:
+                for s in range(PASSES2):
+                    quantise_w_fc1(s)
+
+        reciprocal_std(LAST - 1)
+        for z in range(LAST - 3, LAST + 1):
+            for b in range(2):
+                transpose_z(z, 0, b)
+            for b in range(2):
+                transpose_z(z, 1, b, accp, "acc")
+            if z < LAST:
+                for h in range(TILES):
+                    normalise(nc.vector, z + 1, h, slice(0, 4))
+            for s in range(PASSES2):
+                for b in range(2):
+                    empty_z(z, s, b)
+            for h in range(TILES):
+                second_matmul(z - 2, h)
+            for h in range(TILES):
+                gelu(z - 2, h)
+            for s in range(PASSES2):
+                regroup_h(z - 1, s)
+            quantise_h(z - 1)
+            if z == LAST - 3:
+                var_plus_eps(LAST)
+                reciprocal_std(LAST)
         for s in range(PASSES2):
-            regroup_h(LAST - 1, s)
-        quantise_h(LAST - 1)
-        for b in range(2):
-            transpose_z(LAST, 0, b)
-        for b in range(2):
-            transpose_z(LAST, 1, b)
-        for b in range(2):
-            empty_z(LAST, 0, b)
-        for b in range(2):
-            empty_z(LAST, 1, b)
+            regroup_h(LAST, s)
         for h in range(TILES):
             second_matmul(LAST - 1, h)
             gelu(LAST - 1, h)
-        for s in range(PASSES2):
-            regroup_h(LAST, s)
         quantise_h(LAST)
         for h in range(TILES):
             second_matmul(LAST, h)

@@ -97,6 +97,14 @@ def tile_minitransformerlayer_pb_t_kernel(tc, h_attn, x, w_out, w_fc1, g2, b2, o
         load_h_attn(2)
         load_x(2)
 
+        zeros = const.tile([P, BANK], BF16)
+        nc.vector.memset(zeros[:], 0.0)
+
+        def warm_up(count):
+            for i in range(count):
+                idle = accp.tile([P, BANK], F32, tag="acc", name="idle")
+                nc.tensor.matmul(idle[:], lhsT=zeros[:, 0:P], rhs=zeros[:], start=True, stop=True)
+
         ident_f32 = const.tile([P, P], F32)
         make_identity(nc, ident_f32[:])
         ident_bf = const.tile([P, P], BF16)
@@ -365,13 +373,19 @@ def tile_minitransformerlayer_pb_t_kernel(tc, h_attn, x, w_out, w_fc1, g2, b2, o
             elif h == TILES - 1:
                 nc.sync.dma_start(out=group_view(act_rows, k), in_=act_tiles[k][:])
 
+        warm_up(3)
         transpose_h_attn(0)
         copy_h_attn(0)
+        warm_up(1)
         transpose_w_out(0)
+        warm_up(1)
         transpose_w_out(1)
+        warm_up(1)
         quantise_h_attn(0)
         transpose_w_out(2)
+        warm_up(1)
         transpose_w_out(3)
+        warm_up(1)
         quantise_w_out(0)
         for h in range(TILES):
             first_matmul(0, h, 0)
@@ -397,7 +411,7 @@ def tile_minitransformerlayer_pb_t_kernel(tc, h_attn, x, w_out, w_fc1, g2, b2, o
                 reciprocal_std(k - 2)
             if n >= 0:
                 normalise(nc.gpsimd, n, 0, slice(0, 4))
-                normalise(nc.gpsimd, n, 1, slice(0, 3))
+                normalise(nc.gpsimd, n, 1, slice(0, 2))
 
             if z >= 0:
                 for b in range(2):
@@ -451,7 +465,7 @@ def tile_minitransformerlayer_pb_t_kernel(tc, h_attn, x, w_out, w_fc1, g2, b2, o
                 gelu(m, 1)
 
             if n >= 0:
-                normalise(nc.vector, n, 1, slice(3, 4))
+                normalise(nc.vector, n, 1, slice(2, 4))
             if r >= 0:
                 regroup_h(r, 0)
                 regroup_h(r, 1)

@@ -41,7 +41,7 @@ def tile_minitransformerlayer_pb_t_kernel(tc, h_attn, x, w_out, w_fc1, g2, b2, o
     act_rows = out_1.flatten_outer_dims()
 
     with ExitStack() as ctx:
-        ctx.enter_context(tc.manual_schedule())
+        ctx.enter_context(tc.manual_schedule(engines={mybir.EngineType.PE, mybir.EngineType.DVE, mybir.EngineType.Pool, mybir.EngineType.SP}))
         const = ctx.enter_context(tc.tile_pool(name="const", bufs=1))
         loads = ctx.enter_context(tc.tile_pool(name="loads", bufs=LOADS_AHEAD + 1))
         work = ctx.enter_context(tc.tile_pool(name="work", bufs=2))
@@ -315,18 +315,19 @@ def tile_minitransformerlayer_pb_t_kernel(tc, h_attn, x, w_out, w_fc1, g2, b2, o
                     )
             z_banks[(k, s, b)] = z_ps
 
-        def empty_z(k, s, b):
+        def empty_z(k, s, b, on_vector=False):
             if s == 0 and b == 0:
                 plane_tiles[k] = work.tile([P, D_BLOCKS, GROUP], BF16, name="planes")
             for cc in range(2):
                 t = 2 * b + cc
-                nc.scalar.activation(
-                    out=plane_tiles[k][:, 4 * s + t, :],
-                    in_=z_banks[(k, s, b)][:, cc, :],
-                    func=ACT.Identity,
-                    bias=gb[:, t, PASSES2 + s : PASSES2 + s + 1],
-                    scale=gb[:, t, s : s + 1],
-                )
+                plane = plane_tiles[k][:, 4 * s + t, :]
+                bank = z_banks[(k, s, b)][:, cc, :]
+                gain = gb[:, t, s : s + 1]
+                shift = gb[:, t, PASSES2 + s : PASSES2 + s + 1]
+                if on_vector:
+                    nc.vector.tensor_scalar(out=plane, in0=bank, scalar1=gain, scalar2=shift, op0=ALU.mult, op1=ALU.add)
+                else:
+                    nc.scalar.activation(out=plane, in_=bank, func=ACT.Identity, bias=shift, scale=gain)
 
         def regroup_h(k, s):
             if s == 0:
@@ -336,15 +337,27 @@ def tile_minitransformerlayer_pb_t_kernel(tc, h_attn, x, w_out, w_fc1, g2, b2, o
                 in_=plane_tiles[k][:, 4 * s : 4 * s + 4, :].rearrange("p t (c i) -> p c t i", i=4),
             )
 
-        def quantise_h(k):
+        def start_codes(k):
             z_codes = work.tile([P, PASSES2, GROUP], U32, align_bytes=64, name="z_codes", bufs=3)
             z_scales = work.tile([P, PASSES2, GROUP], U8, align_bytes=64, name="z_scales", bufs=3)
+            z_ops[k] = (z_codes, z_scales)
+            return z_codes, z_scales
+
+        def quantise_h(k):
+            z_codes, z_scales = start_codes(k)
             nc.vector.quantize_mx(
                 out=z_codes[:].rearrange("p s r -> p (s r)").bitcast(FP8X4),
                 scales=z_scales[:].rearrange("p s r -> p (s r)"),
                 in_=zgrp_tiles[k][:].rearrange("p s r t -> p (s r t)"),
             )
-            z_ops[k] = (z_codes, z_scales)
+
+        def quantise_h_pass(k, s):
+            z_codes, z_scales = start_codes(k) if s == 0 else z_ops[k]
+            nc.vector.quantize_mx(
+                out=z_codes[:, s, :].bitcast(FP8X4),
+                scales=z_scales[:, s, :],
+                in_=zgrp_tiles[k][:, s, :, :].rearrange("p r t -> p (r t)"),
+            )
 
         acc2_banks = {}
 
@@ -495,9 +508,11 @@ def tile_minitransformerlayer_pb_t_kernel(tc, h_attn, x, w_out, w_fc1, g2, b2, o
             if z < LAST:
                 for h in range(TILES):
                     normalise(nc.vector, z + 1, h, slice(0, 4))
-            for s in range(PASSES2):
-                for b in range(2):
-                    empty_z(z, s, b)
+            for b in range(2):
+                empty_z(z, 0, b)
+            empty_z(z, 1, 0)
+            if z < LAST:
+                empty_z(z, 1, 1)
             for h in range(TILES):
                 second_matmul(z - 2, h)
             for h in range(TILES):
@@ -508,12 +523,14 @@ def tile_minitransformerlayer_pb_t_kernel(tc, h_attn, x, w_out, w_fc1, g2, b2, o
             if z == LAST - 3:
                 var_plus_eps(LAST)
                 reciprocal_std(LAST)
-        for s in range(PASSES2):
-            regroup_h(LAST, s)
+        empty_z(LAST, 1, 1, on_vector=True)
         for h in range(TILES):
             second_matmul(LAST - 1, h)
             gelu(LAST - 1, h)
-        quantise_h(LAST)
+        for s in range(PASSES2):
+            regroup_h(LAST, s)
+        for s in range(PASSES2):
+            quantise_h_pass(LAST, s)
         for h in range(TILES):
             second_matmul(LAST, h)
             gelu(LAST, h)

@@ -130,7 +130,7 @@ def tile_minitransformerlayer_pb_t_kernel(tc, h_attn, x, w_out, w_fc1, g2, b2, o
                     words = w1_words[:, row * (E // 2) + u : (row + 1) * (E // 2) : 2]
                     nc.tensor.transpose(w1_ps[:, u, rr * P : (rr + 1) * P], words, ident_f32[:])
             w1_out = w1_grp_words[:, q * 2 * P : (q + 1) * 2 * P, :]
-            if q % 2 == 0:
+            if q == 0:
                 nc.vector.tensor_copy(out=w1_out, in_=w1_ps[:].rearrange("p u d -> p d u"))
             else:
                 nc.scalar.copy(out=w1_out, in_=w1_ps[:].rearrange("p u d -> p d u"))
@@ -161,10 +161,15 @@ def tile_minitransformerlayer_pb_t_kernel(tc, h_attn, x, w_out, w_fc1, g2, b2, o
         w2_scales = const.tile([P, PASSES2, F], U8, align_bytes=64)
 
         def permute_w_fc1():
-            nc.vector.tensor_copy(
-                out=w2_perm[:].rearrange("p t f s (q r) -> p t (f s q) r", r=RUN),
-                in_=w2_raw[:].rearrange("p (g t r) -> p t g r", t=4, r=RUN),
-            )
+            for t in range(4):
+                nc.gpsimd.tensor_scalar(
+                    out=w2_perm[:].rearrange("p t f s (q r) -> p t (f s q) r", r=RUN)[:, t, :, :],
+                    in0=w2_raw[:].rearrange("p (g t r) -> p t g r", t=4, r=RUN)[:, t, :, :],
+                    scalar1=1.0,
+                    scalar2=0.0,
+                    op0=ALU.mult,
+                    op1=ALU.add,
+                )
 
         def transpose_w_fc1(s, q):
             w2_ps = ztp.tile([P, 4, 2 * P], BF16, tag="ztp")
@@ -378,7 +383,7 @@ def tile_minitransformerlayer_pb_t_kernel(tc, h_attn, x, w_out, w_fc1, g2, b2, o
 
         def gelu(k, h):
             if h == 0:
-                act_tiles[k] = work.tile([P, TILES, F], F32, name="act", bufs=3)
+                act_tiles[k] = work.tile([P, TILES, F], F32, name="act", bufs=4)
             nc.scalar.activation(out=act_tiles[k][:, h, :], in_=acc2_banks[(k, h)][:], func=ACT.Gelu)
             if k == LAST:
                 j = (k % 2) * TILES + h
@@ -395,16 +400,16 @@ def tile_minitransformerlayer_pb_t_kernel(tc, h_attn, x, w_out, w_fc1, g2, b2, o
         transpose_w_out(1)
         warm_up(1)
         quantise_h_attn(0)
+        quantise_w_out(0)
         transpose_w_out(2)
         warm_up(1)
         transpose_w_out(3)
         warm_up(1)
-        quantise_w_out(0)
+        quantise_w_out(1)
         for h in range(TILES):
             first_matmul(0, h, 0)
         transpose_h_attn(1)
         copy_h_attn(1)
-        quantise_w_out(1)
         for h in range(TILES):
             first_matmul(0, h, 1)
         transpose_h_attn(2)
@@ -433,17 +438,17 @@ def tile_minitransformerlayer_pb_t_kernel(tc, h_attn, x, w_out, w_fc1, g2, b2, o
             if k == 0:
                 add_residual(0, 0, 0)
                 add_residual(0, 1, 0)
+                add_residual(0, 0, 1)
+                add_residual(0, 1, 1)
             else:
                 add_residual(k, 0, 0)
             if m >= 0:
                 second_matmul(m, 0)
             if k == 0:
+                minus_mean(0, 0)
                 quantise_h_attn(1)
                 first_matmul(1, 0, 0)
                 first_matmul(1, 0, 1)
-                add_residual(0, 0, 1)
-                add_residual(0, 1, 1)
-                minus_mean(0, 0)
                 first_matmul(1, 1, 0)
                 first_matmul(1, 1, 1)
             else:
@@ -477,11 +482,11 @@ def tile_minitransformerlayer_pb_t_kernel(tc, h_attn, x, w_out, w_fc1, g2, b2, o
             if m >= 0:
                 gelu(m, 1)
 
-            if n >= 0:
-                normalise(nc.vector, n, 1, slice(2, 4))
             if r >= 0:
                 regroup_h(r, 0)
                 regroup_h(r, 1)
+            if n >= 0:
+                normalise(nc.vector, n, 1, slice(2, 4))
             if live(k + 2):
                 quantise_h_attn(k + 2)
             if r >= 0:
@@ -495,9 +500,8 @@ def tile_minitransformerlayer_pb_t_kernel(tc, h_attn, x, w_out, w_fc1, g2, b2, o
                     transpose_w_fc1(k - 1, q)
             if k == 1:
                 transpose_gain_and_bias()
-            if k == 3:
-                for s in range(PASSES2):
-                    quantise_w_fc1(s)
+            if k == 3 or k == 4:
+                quantise_w_fc1(k - 3)
 
         reciprocal_std(LAST - 1)
         for z in range(LAST - 3, LAST + 1):
@@ -506,12 +510,11 @@ def tile_minitransformerlayer_pb_t_kernel(tc, h_attn, x, w_out, w_fc1, g2, b2, o
             for b in range(2):
                 transpose_z(z, 1, b, accp, "acc")
             if z < LAST:
-                for h in range(TILES):
-                    normalise(nc.vector, z + 1, h, slice(0, 4))
+                normalise(nc.vector, z + 1, 0, slice(0, 4))
             for b in range(2):
                 empty_z(z, 0, b)
             empty_z(z, 1, 0)
-            if z < LAST:
+            if z < LAST - 1:
                 empty_z(z, 1, 1)
             for h in range(TILES):
                 second_matmul(z - 2, h)
@@ -519,11 +522,14 @@ def tile_minitransformerlayer_pb_t_kernel(tc, h_attn, x, w_out, w_fc1, g2, b2, o
                 gelu(z - 2, h)
             for s in range(PASSES2):
                 regroup_h(z - 1, s)
+            if z < LAST:
+                normalise(nc.vector, z + 1, 1, slice(0, 4))
             quantise_h(z - 1)
+            if z >= LAST - 1:
+                empty_z(z, 1, 1, on_vector=True)
             if z == LAST - 3:
                 var_plus_eps(LAST)
                 reciprocal_std(LAST)
-        empty_z(LAST, 1, 1, on_vector=True)
         for h in range(TILES):
             second_matmul(LAST - 1, h)
             gelu(LAST - 1, h)

@@ -82,10 +82,11 @@ def tile_minitransformerlayer_pb_t_kernel(tc, h_attn, x, w_out, w_fc1, g2, b2, o
         def load_first(tile, rows, k):
             nc.sync.dma_start(out=tile[:, group_tiles(k), :], in_=group_view(rows, k))
 
-        load_first(ha_tiles[0], ha_rows, 0)
         for q in range(D_BLOCKS // 2):
             two = slice(2 * q, 2 * q + 2)
             nc.sync.dma_start(out=w1_raw[:, two, :], in_=w_out_blocks[:, two, :])
+            if q == 0:
+                load_first(ha_tiles[0], ha_rows, 0)
         load_first(x_tiles[0], x_rows, 0)
         load_first(ha_tiles[0], ha_rows, 1)
         load_first(x_tiles[0], x_rows, 1)
@@ -155,29 +156,36 @@ def tile_minitransformerlayer_pb_t_kernel(tc, h_attn, x, w_out, w_fc1, g2, b2, o
                 nc.tensor.transpose(gb_ps[:, t, :], gb_perm[:, t, :], ident_bf[:])
             nc.scalar.copy(out=gb[:], in_=gb_ps[:, :, 0 : 2 * PASSES2])
 
-        w2_perm = const.tile([P, 4, F // P, PASSES2, P], BF16)
+        w2_perm = const.tile([P, 2, F // P, PASSES2, 2 * P], BF16)
         w2_grp = const.tile([P, PASSES2, F, 4], BF16, align_bytes=64)
         w2_codes = const.tile([P, PASSES2, F], U32, align_bytes=64)
         w2_scales = const.tile([P, PASSES2, F], U8, align_bytes=64)
 
         def permute_w_fc1():
-            for t in range(4):
-                nc.gpsimd.tensor_scalar(
-                    out=w2_perm[:].rearrange("p t f s (q r) -> p t (f s q) r", r=RUN)[:, t, :, :],
-                    in0=w2_raw[:].rearrange("p (g t r) -> p t g r", t=4, r=RUN)[:, t, :, :],
-                    scalar1=1.0,
-                    scalar2=0.0,
-                    op0=ALU.mult,
-                    op1=ALU.add,
-                )
+            rows = F // P // 2
+            for half in range(2):
+                for u in range(2):
+                    nc.gpsimd.tensor_scalar(
+                        out=w2_perm[:, u, half * rows : (half + 1) * rows, :, :].rearrange(
+                            "p f s (q r e) -> p (f s q) r e", r=RUN, e=2
+                        ),
+                        in0=w2_raw[:, half * rows * D : (half + 1) * rows * D].rearrange(
+                            "p (g u e r) -> p u g r e", u=2, e=2, r=RUN
+                        )[:, u, :, :, :],
+                        scalar1=1.0,
+                        scalar2=0.0,
+                        op0=ALU.mult,
+                        op1=ALU.add,
+                    )
 
         def transpose_w_fc1(s, q):
-            w2_ps = ztp.tile([P, 4, 2 * P], BF16, tag="ztp")
-            for t in range(4):
+            w2_ps = ztp.tile([P, 2, 2 * P], F32, tag="ztp")
+            for u in range(2):
                 for rr in range(2):
-                    nc.tensor.transpose(w2_ps[:, t, rr * P : (rr + 1) * P], w2_perm[:, t, 2 * q + rr, s, :], ident_bf[:])
-            w2_out = w2_grp[:, s, q * 2 * P : (q + 1) * 2 * P, :]
-            nc.scalar.copy(out=w2_out, in_=w2_ps[:].rearrange("p t f -> p f t"))
+                    words = w2_perm[:, u, 2 * q + rr, s, :].bitcast(F32)
+                    nc.tensor.transpose(w2_ps[:, u, rr * P : (rr + 1) * P], words, ident_f32[:])
+            w2_out = w2_grp[:, s, q * 2 * P : (q + 1) * 2 * P, :].rearrange("p f t -> p (f t)").bitcast(F32)
+            nc.scalar.copy(out=w2_out.rearrange("p (f u) -> p f u", u=2), in_=w2_ps[:].rearrange("p u f -> p f u"))
 
         def quantise_w_fc1(s):
             nc.vector.quantize_mx(
@@ -216,7 +224,7 @@ def tile_minitransformerlayer_pb_t_kernel(tc, h_attn, x, w_out, w_fc1, g2, b2, o
             h_groups[k] = work.tile([P, GROUP * 4], BF16, align_bytes=64, name="h_grp", bufs=3)
             out = h_groups[k][:].bitcast(F32).rearrange("p (r u) -> p r u", u=2)
             in_ = h_banks[k][:].rearrange("p u r -> p r u")
-            if k < 3:
+            if k < 4:
                 nc.scalar.copy(out=out, in_=in_)
             else:
                 nc.vector.tensor_copy(out=out, in_=in_)
@@ -391,11 +399,10 @@ def tile_minitransformerlayer_pb_t_kernel(tc, h_attn, x, w_out, w_fc1, g2, b2, o
             elif h == TILES - 1:
                 nc.sync.dma_start(out=group_view(act_rows, k), in_=act_tiles[k][:])
 
-        warm_up(3)
+        warm_up(6)
+        transpose_w_out(0)
         transpose_h_attn(0)
         copy_h_attn(0)
-        warm_up(1)
-        transpose_w_out(0)
         warm_up(1)
         transpose_w_out(1)
         warm_up(1)
@@ -435,6 +442,8 @@ def tile_minitransformerlayer_pb_t_kernel(tc, h_attn, x, w_out, w_fc1, g2, b2, o
                 for b in range(2):
                     transpose_z(z, 0, b)
                     empty_z(z, 0, b)
+            if k == 1:
+                copy_h_attn(k + 2)
             if k == 0:
                 add_residual(0, 0, 0)
                 add_residual(0, 1, 0)
@@ -464,7 +473,7 @@ def tile_minitransformerlayer_pb_t_kernel(tc, h_attn, x, w_out, w_fc1, g2, b2, o
             if k > 0:
                 add_residual(k, 1, 1)
             store_xmid(k)
-            if k > 0 and live(k + 2):
+            if k > 0 and live(k + 2) and k > 1:
                 copy_h_attn(k + 2)
             minus_mean(k, 1)
             variance(k, 1)

from contextlib import ExitStack

import concourse.mybir as mybir
from concourse.masks import make_identity

F32 = mybir.dt.float32
BF16 = mybir.dt.bfloat16
U32 = mybir.dt.uint32
U8 = mybir.dt.uint8
FP8X4 = mybir.dt.float8_e4m3fn_x4
ACT = mybir.ActivationFunctionType
ALU = mybir.AluOpType

P = 128
TOKENS = 4096
D = 1024
E = 512
F = 512
EPS = 1e-5
BANK = 512
D_BLOCKS = D // P
PASSES2 = D // 512
RUN = 8
LOAD_TILES = 4
LOAD_TOKENS = LOAD_TILES * P
LOADS = TOKENS // LOAD_TOKENS
TILES = 2
GROUP = TILES * P
GROUPS = TOKENS // GROUP
LAST = GROUPS - 1
LOADS_AHEAD = 3

FLOPS = 2 * TOKENS * E * D + 2 * TOKENS * D * F


def tile_minitransformerlayer_pb_t_kernel(tc, h_attn, x, w_out, w_fc1, g2, b2, out_0, out_1):
    nc = tc.nc
    ha_rows = h_attn.flatten_outer_dims()
    x_rows = x.flatten_outer_dims()
    xmid_rows = out_0.flatten_outer_dims()
    act_rows = out_1.flatten_outer_dims()

    with ExitStack() as ctx:
        ctx.enter_context(tc.manual_schedule(engines={mybir.EngineType.PE, mybir.EngineType.DVE, mybir.EngineType.Pool, mybir.EngineType.SP}))
        const = ctx.enter_context(tc.tile_pool(name="const", bufs=1))
        loads = ctx.enter_context(tc.tile_pool(name="loads", bufs=LOADS_AHEAD + 1))
        work = ctx.enter_context(tc.tile_pool(name="work", bufs=2))
        small = ctx.enter_context(tc.tile_pool(name="small", bufs=6))
        accp = ctx.enter_context(tc.psum_pool(name="accp", bufs=5))
        ztp = ctx.enter_context(tc.psum_pool(name="ztp", bufs=2))
        htp = ctx.enter_context(tc.psum_pool(name="htp", bufs=1))

        def load_view(rows, n):
            return rows[n * LOAD_TOKENS : (n + 1) * LOAD_TOKENS, :].rearrange("(p j) c -> p j c", j=LOAD_TILES)

        def group_tiles(k):
            first = (k % 2) * TILES
            return slice(first, first + TILES)

        def group_view(rows, k):
            return load_view(rows, k // 2)[:, group_tiles(k), :]

        ha_tiles = {}
        x_tiles = {}

        def load_h_attn(n):
            ha_tiles[n] = loads.tile([P, LOAD_TILES, E], BF16, name="ha_sb")
            nc.sync.dma_start(out=ha_tiles[n][:], in_=load_view(ha_rows, n))

        def load_x(n):
            x_tiles[n] = loads.tile([P, LOAD_TILES, D], BF16, name="x_sb")
            nc.sync.dma_start(out=x_tiles[n][:], in_=load_view(x_rows, n))

        w1_raw = const.tile([P, D_BLOCKS, E], BF16)
        w_out_blocks = w_out.rearrange("(r p) k -> p r k", p=P)
        w2_raw = const.tile([P, F // P * D], BF16)
        gb_rows = const.tile([P, PASSES2 * 256], BF16)
        nc.vector.memset(gb_rows[:], 0.0)
        ha_tiles[0] = loads.tile([P, LOAD_TILES, E], BF16, name="ha_sb")
        x_tiles[0] = loads.tile([P, LOAD_TILES, D], BF16, name="x_sb")

        def load_first(tile, rows, k):
            nc.sync.dma_start(out=tile[:, group_tiles(k), :], in_=group_view(rows, k))

        for q in range(D_BLOCKS // 2):
            two = slice(2 * q, 2 * q + 2)
            nc.sync.dma_start(out=w1_raw[:, two, :], in_=w_out_blocks[:, two, :])
            if q == 0:
                load_first(ha_tiles[0], ha_rows, 0)
        load_first(x_tiles[0], x_rows, 0)
        load_first(ha_tiles[0], ha_rows, 1)
        load_first(x_tiles[0], x_rows, 1)
        load_h_attn(1)
        nc.sync.dma_start(out=w2_raw[:].rearrange("p (r k) -> p r k", k=D), in_=w_fc1.rearrange("(r p) k -> p r k", p=P))
        load_x(1)
        nc.sync.dma_start(out=gb_rows[0:PASSES2, :], in_=g2.rearrange("(s k) -> s k", k=512))
        nc.sync.dma_start(out=gb_rows[PASSES2 : 2 * PASSES2, :], in_=b2.rearrange("(s k) -> s k", k=512))
        load_h_attn(2)
        load_x(2)

        zeros = const.tile([P, BANK], BF16)
        nc.vector.memset(zeros[:], 0.0)

        def warm_up(count):
            for i in range(count):
                idle = accp.tile([P, BANK], F32, tag="acc", name="idle")
                nc.tensor.matmul(idle[:], lhsT=zeros[:, 0:P], rhs=zeros[:], start=True, stop=True)

        ident_f32 = const.tile([P, P], F32)
        make_identity(nc, ident_f32[:])
        ident_bf = const.tile([P, P], BF16)
        make_identity(nc, ident_bf[:])
        neg_half = const.tile([P, TILES], F32)
        nc.gpsimd.memset(neg_half[:], -0.5)
        warm = const.tile([P, 1], F32)
        nc.vector.memset(warm[:], 0.0)
        nc.scalar.activation(out=warm[:], in_=warm[:], func=ACT.Gelu)

        w1_grp = const.tile([P, D * 4], BF16, align_bytes=64)
        w1_grp_words = w1_grp[:].bitcast(F32).rearrange("p (d u) -> p d u", u=2)
        w1_codes = const.tile([P, D], U32, align_bytes=64)
        w1_scales = const.tile([P, D], U8, align_bytes=64)

        def transpose_w_out(q):
            w1_words = w1_raw[:].rearrange("p r k -> p (r k)").bitcast(F32)
            pool, tag = (ztp, "ztp") if q < 2 else (accp, "acc")
            w1_ps = pool.tile([P, 2, 2 * P], F32, tag=tag, name="w1_ps")
            for rr in range(2):
                for u in range(2):
                    row = 2 * q + rr
                    words = w1_words[:, row * (E // 2) + u : (row + 1) * (E // 2) : 2]
                    nc.tensor.transpose(w1_ps[:, u, rr * P : (rr + 1) * P], words, ident_f32[:])
            w1_out = w1_grp_words[:, q * 2 * P : (q + 1) * 2 * P, :]
            if q == 0:
                nc.vector.tensor_copy(out=w1_out, in_=w1_ps[:].rearrange("p u d -> p d u"))
            else:
                nc.scalar.copy(out=w1_out, in_=w1_ps[:].rearrange("p u d -> p d u"))

        def quantise_w_out(half):
            nc.vector.quantize_mx(
                out=w1_codes[:, half * BANK : (half + 1) * BANK].bitcast(FP8X4),
                scales=w1_scales[:, half * BANK : (half + 1) * BANK],
                in_=w1_grp[:, half * BANK * 4 : (half + 1) * BANK * 4],
            )

        gb = const.tile([P, 4, 2 * PASSES2], F32)

        def transpose_gain_and_bias():
            gb_perm = const.tile([P, 4, P], BF16)
            nc.vector.tensor_copy(
                out=gb_perm[:].rearrange("p t (q r) -> p t q r", r=RUN),
                in_=gb_rows[:].rearrange("p (q t r) -> p t q r", t=4, r=RUN),
            )
            gb_ps = ztp.tile([P, 4, P], BF16, tag="ztp")
            for t in range(4):
                nc.tensor.transpose(gb_ps[:, t, :], gb_perm[:, t, :], ident_bf[:])
            nc.scalar.copy(out=gb[:], in_=gb_ps[:, :, 0 : 2 * PASSES2])

        w2_perm = const.tile([P, 2, F // P, PASSES2, 2 * P], BF16)
        w2_grp = const.tile([P, PASSES2, F, 4], BF16, align_bytes=64)
        w2_codes = const.tile([P, PASSES2, F], U32, align_bytes=64)
        w2_scales = const.tile([P, PASSES2, F], U8, align_bytes=64)

        def permute_w_fc1():
            rows = F // P // 2
            for half in range(2):
                for u in range(2):
                    nc.gpsimd.tensor_scalar(
                        out=w2_perm[:, u, half * rows : (half + 1) * rows, :, :].rearrange(
                            "p f s (q r e) -> p (f s q) r e", r=RUN, e=2
                        ),
                        in0=w2_raw[:, half * rows * D : (half + 1) * rows * D].rearrange(
                            "p (g u e r) -> p u g r e", u=2, e=2, r=RUN
                        )[:, u, :, :, :],
                        scalar1=1.0,
                        scalar2=0.0,
                        op0=ALU.mult,
                        op1=ALU.add,
                    )

        def transpose_w_fc1(s, q):
            w2_ps = ztp.tile([P, 2, 2 * P], F32, tag="ztp")
            for u in range(2):
                for rr in range(2):
                    words = w2_perm[:, u, 2 * q + rr, s, :].bitcast(F32)
                    nc.tensor.transpose(w2_ps[:, u, rr * P : (rr + 1) * P], words, ident_f32[:])
            w2_out = w2_grp[:, s, q * 2 * P : (q + 1) * 2 * P, :].rearrange("p f t -> p (f t)").bitcast(F32)
            nc.scalar.copy(out=w2_out.rearrange("p (f u) -> p f u", u=2), in_=w2_ps[:].rearrange("p u f -> p f u"))

        def quantise_w_fc1(s):
            nc.vector.quantize_mx(
                out=w2_codes[:, s, :].bitcast(FP8X4),
                scales=w2_scales[:, s, :],
                in_=w2_grp[:, s, :, :].rearrange("p f t -> p (f t)"),
            )

        h_banks = {}
        h_groups = {}
        h_ops = {}
        acc1_banks = {}
        xm_tiles = {}
        mean_tiles = {}
        z_tiles = {}
        z_banks = {}
        norm_tiles = {}
        plane_tiles = {}
        zgrp_tiles = {}
        z_ops = {}
        act_tiles = {}

        def live(k):
            return 0 <= k < GROUPS

        def transpose_h_attn(k):
            h_banks[k] = htp.tile([P, 2, GROUP], F32, name="h_ps")
            ha_words = ha_tiles[k // 2][:].rearrange("p j c -> p (j c)").bitcast(F32)
            for h in range(TILES):
                for u in range(2):
                    row = (k % 2) * TILES + h
                    words = ha_words[:, row * (E // 2) + u : (row + 1) * (E // 2) : 2]
                    nc.tensor.transpose(h_banks[k][:, u, h * P : (h + 1) * P], words, ident_f32[:])

        def copy_h_attn(k):
            h_groups[k] = work.tile([P, GROUP * 4], BF16, align_bytes=64, name="h_grp", bufs=3)
            out = h_groups[k][:].bitcast(F32).rearrange("p (r u) -> p r u", u=2)
            in_ = h_banks[k][:].rearrange("p u r -> p r u")
            if k < 4:
                nc.scalar.copy(out=out, in_=in_)
            else:
                nc.vector.tensor_copy(out=out, in_=in_)

        def quantise_h_attn(k):
            h_codes = work.tile([P, GROUP], U32, align_bytes=64, name="h_codes", bufs=4)
            h_scales = work.tile([P, GROUP], U8, align_bytes=64, name="h_scales", bufs=4)
            nc.vector.quantize_mx(out=h_codes[:].bitcast(FP8X4), scales=h_scales[:], in_=h_groups[k][:])
            h_ops[k] = (h_codes, h_scales)

        def first_matmul(k, h, half):
            h_codes, h_scales = h_ops[k]
            tok = slice(h * P, (h + 1) * P)
            cols = slice(half * BANK, (half + 1) * BANK)
            acc1 = accp.tile([P, BANK], F32, tag="acc")
            nc.tensor.matmul_mx(
                out=acc1[:],
                lhsT=h_codes[:, tok].bitcast(FP8X4),
                lhsT_scale=h_scales[:, tok],
                rhs=w1_codes[:, cols].bitcast(FP8X4),
                rhs_scale=w1_scales[:, cols],
                start=True,
                stop=True,
            )
            acc1_banks[(k, h, half)] = acc1

        def start_group(k):
            xm_tiles[k] = work.tile([P, TILES, D], F32, name="xm", bufs=5)
            mean_tiles[k] = (small.tile([P, TILES, 2], F32, name="sums"), small.tile([P, TILES], F32, name="neg_mu"))
            norm_tiles[k] = (
                small.tile([P, TILES], F32, name="ssq"),
                small.tile([P, TILES], F32, name="var_eps"),
                small.tile([P, TILES], F32, name="rstd"),
            )

        def add_residual(k, h, half):
            cols = slice(half * BANK, (half + 1) * BANK)
            nc.vector.scalar_tensor_tensor(
                out=xm_tiles[k][:, h, cols],
                in0=acc1_banks[(k, h, half)][:],
                scalar=1.0,
                in1=x_tiles[k // 2][:, (k % 2) * TILES + h, cols],
                op0=ALU.mult,
                op1=ALU.add,
                accum_out=mean_tiles[k][0][:, h, half : half + 1],
            )

        def store_xmid(k):
            nc.sync.dma_start(out=group_view(xmid_rows, k), in_=xm_tiles[k][:])

        def minus_mean(k, h):
            sums, neg_mu = mean_tiles[k]
            nc.vector.tensor_scalar(
                out=neg_mu[:, h : h + 1],
                in0=sums[:, h, 0:1],
                scalar1=sums[:, h, 1:2],
                scalar2=-1.0 / D,
                op0=ALU.add,
                op1=ALU.mult,
            )

        def variance(k, h):
            one = slice(h, h + 1)
            squares = work.tile([P, D], BF16, name="squares")
            nc.scalar.activation(
                out=squares[:],
                in_=xm_tiles[k][:, h, :],
                func=ACT.Square,
                bias=mean_tiles[k][1][:, one],
                scale=1.0,
                accum_out=norm_tiles[k][0][:, one],
            )

        def var_plus_eps(k):
            ssq, var_eps, rstd = norm_tiles[k]
            nc.vector.tensor_scalar(out=var_eps[:], in0=ssq[:], scalar1=1.0 / D, scalar2=EPS, op0=ALU.mult, op1=ALU.add)

        def reciprocal_std(k):
            ssq, var_eps, rstd = norm_tiles[k]
            nc.gpsimd.tensor_tensor(out=rstd[:], in0=var_eps[:], in1=neg_half[:], op=ALU.pow)

        def normalise(engine, k, h, blocks):
            if k not in z_tiles:
                z_tiles[k] = work.tile([P, TILES, 4, D // 4], F32, name="z", bufs=3)
            one = slice(h, h + 1)
            engine.tensor_scalar(
                out=z_tiles[k][:, h, blocks, :].rearrange("p t (g r) -> p t g r", r=RUN),
                in0=xm_tiles[k][:, h, :].rearrange("p (g t r) -> p t g r", t=4, r=RUN)[:, blocks, :, :],
                scalar1=mean_tiles[k][1][:, one],
                scalar2=norm_tiles[k][2][:, one],
                op0=ALU.add,
                op1=ALU.mult,
            )

        def transpose_z(k, s, b, pool=ztp, tag="ztp"):
            z_ps = pool.tile([P, 2, GROUP], F32, tag=tag, name="z_ps")
            for cc in range(2):
                for j in range(TILES):
                    nc.tensor.transpose(
                        z_ps[:, cc, j * P : (j + 1) * P], z_tiles[k][:, j, 2 * b + cc, s * P : (s + 1) * P], ident_f32[:]
                    )
            z_banks[(k, s, b)] = z_ps

        def empty_z(k, s, b, on_vector=False):
            if s == 0 and b == 0:
                plane_tiles[k] = work.tile([P, D_BLOCKS, GROUP], BF16, name="planes")
            for cc in range(2):
                t = 2 * b + cc
                plane = plane_tiles[k][:, 4 * s + t, :]
                bank = z_banks[(k, s, b)][:, cc, :]
                gain = gb[:, t, s : s + 1]
                shift = gb[:, t, PASSES2 + s : PASSES2 + s + 1]
                if on_vector:
                    nc.vector.tensor_scalar(out=plane, in0=bank, scalar1=gain, scalar2=shift, op0=ALU.mult, op1=ALU.add)
                else:
                    nc.scalar.activation(out=plane, in_=bank, func=ACT.Identity, bias=shift, scale=gain)

        def regroup_h(k, s):
            if s == 0:
                zgrp_tiles[k] = work.tile([P, PASSES2, GROUP, 4], BF16, align_bytes=64, name="z_grp")
            nc.vector.tensor_copy(
                out=zgrp_tiles[k][:, s, :, :].rearrange("p (c i) t -> p c t i", i=4),
                in_=plane_tiles[k][:, 4 * s : 4 * s + 4, :].rearrange("p t (c i) -> p c t i", i=4),
            )

        def start_codes(k):
            z_codes = work.tile([P, PASSES2, GROUP], U32, align_bytes=64, name="z_codes", bufs=3)
            z_scales = work.tile([P, PASSES2, GROUP], U8, align_bytes=64, name="z_scales", bufs=3)
            z_ops[k] = (z_codes, z_scales)
            return z_codes, z_scales

        def quantise_h(k):
            z_codes, z_scales = start_codes(k)
            nc.vector.quantize_mx(
                out=z_codes[:].rearrange("p s r -> p (s r)").bitcast(FP8X4),
                scales=z_scales[:].rearrange("p s r -> p (s r)"),
                in_=zgrp_tiles[k][:].rearrange("p s r t -> p (s r t)"),
            )

        def quantise_h_pass(k, s):
            z_codes, z_scales = start_codes(k) if s == 0 else z_ops[k]
            nc.vector.quantize_mx(
                out=z_codes[:, s, :].bitcast(FP8X4),
                scales=z_scales[:, s, :],
                in_=zgrp_tiles[k][:, s, :, :].rearrange("p r t -> p (r t)"),
            )

        acc2_banks = {}

        def second_matmul(k, h):
            z_codes, z_scales = z_ops[k]
            tok = slice(h * P, (h + 1) * P)
            acc2_banks[(k, h)] = accp.tile([P, F], F32, tag="acc", name="acc2")
            for s in range(PASSES2):
                nc.tensor.matmul_mx(
                    out=acc2_banks[(k, h)][:],
                    lhsT=z_codes[:, s, tok].bitcast(FP8X4),
                    lhsT_scale=z_scales[:, s, tok],
                    rhs=w2_codes[:, s, :].bitcast(FP8X4),
                    rhs_scale=w2_scales[:, s, :],
                    start=(s == 0),
                    stop=(s == PASSES2 - 1),
                )

        def gelu(k, h):
            if h == 0:
                act_tiles[k] = work.tile([P, TILES, F], F32, name="act", bufs=4)
            nc.scalar.activation(out=act_tiles[k][:, h, :], in_=acc2_banks[(k, h)][:], func=ACT.Gelu)
            if k == LAST:
                j = (k % 2) * TILES + h
                nc.sync.dma_start(out=load_view(act_rows, k // 2)[:, j, :], in_=act_tiles[k][:, h, :])
            elif h == TILES - 1:
                nc.sync.dma_start(out=group_view(act_rows, k), in_=act_tiles[k][:])

        warm_up(6)
        transpose_w_out(0)
        transpose_h_attn(0)
        copy_h_attn(0)
        warm_up(1)
        transpose_w_out(1)
        warm_up(1)
        quantise_h_attn(0)
        quantise_w_out(0)
        transpose_w_out(2)
        warm_up(1)
        transpose_w_out(3)
        warm_up(1)
        quantise_w_out(1)
        for h in range(TILES):
            first_matmul(0, h, 0)
        transpose_h_attn(1)
        copy_h_attn(1)
        for h in range(TILES):
            first_matmul(0, h, 1)
        transpose_h_attn(2)
        copy_h_attn(2)

        for k in range(GROUPS):
            n = k - 3
            z = k - 4
            r = k - 5
            m = k - 6
            if k % 2 == 0 and k // 2 + LOADS_AHEAD < LOADS:
                load_h_attn(k // 2 + LOADS_AHEAD)
                load_x(k // 2 + LOADS_AHEAD)
            start_group(k)

            if k >= 2:
                reciprocal_std(k - 2)
            if n >= 0:
                normalise(nc.gpsimd, n, 0, slice(0, 4))
                normalise(nc.gpsimd, n, 1, slice(0, 2))

            if z >= 0:
                for b in range(2):
                    transpose_z(z, 0, b)
                    empty_z(z, 0, b)
            if k == 1:
                copy_h_attn(k + 2)
            if k == 0:
                add_residual(0, 0, 0)
                add_residual(0, 1, 0)
                add_residual(0, 0, 1)
                add_residual(0, 1, 1)
            else:
                add_residual(k, 0, 0)
            if m >= 0:
                second_matmul(m, 0)
            if k == 0:
                minus_mean(0, 0)
                quantise_h_attn(1)
                first_matmul(1, 0, 0)
                first_matmul(1, 0, 1)
                first_matmul(1, 1, 0)
                first_matmul(1, 1, 1)
            else:
                add_residual(k, 0, 1)
                add_residual(k, 1, 0)
                minus_mean(k, 0)
                if k < LAST:
                    first_matmul(k + 1, 0, 0)
                    first_matmul(k + 1, 0, 1)
            variance(k, 0)
            if m >= 0:
                gelu(m, 0)
            if k > 0:
                add_residual(k, 1, 1)
            store_xmid(k)
            if k > 0 and live(k + 2) and k > 1:
                copy_h_attn(k + 2)
            minus_mean(k, 1)
            variance(k, 1)
            if z >= 0:
                for b in range(2):
                    transpose_z(z, 1, b)
                    empty_z(z, 1, b)
            if m >= 0:
                second_matmul(m, 1)
            if 0 < k < LAST:
                first_matmul(k + 1, 1, 0)
                first_matmul(k + 1, 1, 1)
            if live(k + 3):
                transpose_h_attn(k + 3)
            if m >= 0:
                gelu(m, 1)

            if r >= 0:
                regroup_h(r, 0)
                regroup_h(r, 1)
            if n >= 0:
                normalise(nc.vector, n, 1, slice(2, 4))
            if live(k + 2):
                quantise_h_attn(k + 2)
            if r >= 0:
                quantise_h(r)
            if k >= 1:
                var_plus_eps(k - 1)
            if k == 0:
                permute_w_fc1()
            if k == 1 or k == 2:
                for q in range(2):
                    transpose_w_fc1(k - 1, q)
            if k == 1:
                transpose_gain_and_bias()
            if k == 3 or k == 4:
                quantise_w_fc1(k - 3)

        reciprocal_std(LAST - 1)
        for z in range(LAST - 3, LAST + 1):
            for b in range(2):
                transpose_z(z, 0, b)
            for b in range(2):
                transpose_z(z, 1, b, accp, "acc")
            if z < LAST:
                normalise(nc.vector, z + 1, 0, slice(0, 4))
            for b in range(2):
                empty_z(z, 0, b)
            empty_z(z, 1, 0)
            if z < LAST - 1:
                empty_z(z, 1, 1)
            for h in range(TILES):
                second_matmul(z - 2, h)
            for h in range(TILES):
                gelu(z - 2, h)
            for s in range(PASSES2):
                regroup_h(z - 1, s)
            if z < LAST:
                normalise(nc.vector, z + 1, 1, slice(0, 4))
            quantise_h(z - 1)
            if z >= LAST - 1:
                empty_z(z, 1, 1, on_vector=True)
            if z == LAST - 3:
                var_plus_eps(LAST)
                reciprocal_std(LAST)
        for h in range(TILES):
            second_matmul(LAST - 1, h)
            gelu(LAST - 1, h)
        for s in range(PASSES2):
            regroup_h(LAST, s)
        for s in range(PASSES2):
            quantise_h_pass(LAST, s)
        for h in range(TILES):
            second_matmul(LAST, h)
            gelu(LAST, h)
